import numpy as np
import ml_dtypes


def mxq(x, axis, fmt="e4m3"):
    dtype, down = {"e4m3": (ml_dtypes.float8_e4m3fn, 7), "e5m2": (ml_dtypes.float8_e5m2, 14)}[fmt]
    v = np.moveaxis(np.asarray(x, np.float32).astype(ml_dtypes.bfloat16).astype(np.float64), axis, -1)
    blocks = v.reshape(v.shape[:-1] + (-1, 32))
    amax = np.abs(blocks).max(-1, keepdims=True)
    byte = np.maximum(np.where(amax > 0, np.frexp(amax)[1] - 1 + 127, 0) - down, 1)
    scale = np.exp2(byte - 127.0)
    codes = (blocks / scale).astype(np.float32).astype(dtype).astype(np.float64)
    return np.moveaxis((codes * scale).reshape(v.shape), -1, axis)


WIDE = False


def mx_kscale(k):
    if not WIDE:
        return np.ones(k)
    levels = np.array([10, -10, 5, -5, 0])
    a = np.random.permutation(np.resize(levels, k // 512 * 4)).reshape(k // 512, 4)
    idx = np.arange(k)
    return np.exp2(a[idx // 512, idx % 128 // 32])


BF16 = ml_dtypes.bfloat16


def bf(x):
    return np.asarray(x, np.float32).astype(BF16)


def f64(x):
    return np.asarray(x).astype(np.float64)


M, B, I, H, O = 5, 2048, 128, 512, 64
O2 = 2 * O
EPS = 1e-6


def softplus(v):
    return np.maximum(v, 0.0) + np.log(1.0 + np.exp(-np.abs(v)))


def setup_inputs():
    s, t = mx_kscale(H), mx_kscale(H)
    return {"h1": bf(np.maximum(np.random.standard_normal((M, B, H)), 0.0) * s),
            "W2": bf(np.random.standard_normal((M, H, H)) * 1.4 / np.sqrt(H) * t[None, :, None] / s[None, None, :]),
            "b2": bf(np.random.standard_normal((M, H)) * 0.3 * t),
            "W3": bf(np.random.standard_normal((M, O2, H)) * 1.4 / np.sqrt(H) / t[None, None, :]),
            "b3": bf(np.random.standard_normal((M, O2)) * 0.3)}


def reference(h1, W2, b2, W3, b3):
    h2 = np.maximum((mxq(f64(h1), 2, "e4m3") @ mxq(f64(W2), 2, "e4m3").transpose(0, 2, 1)) + f64(b2)[:, None, :], 0.0)
    y = (mxq(h2, 2, "e4m3") @ mxq(f64(W3), 2, "e4m3").transpose(0, 2, 1)) + f64(b3)[:, None, :]
    means = y[:, :, :O]
    variances = softplus(y[:, :, O:]) + EPS
    mean = means.mean(axis=0)
    variance = (variances + means ** 2).mean(axis=0) - mean ** 2
    variance = np.maximum(variance, 0.0) + EPS
    return mean, variance

@@ -1,0 +1,268 @@
+import math
+from contextlib import ExitStack
+
+import concourse.bass as bass
+import concourse.mybir as mybir
+import concourse.tile as tile
+from concourse.masks import make_identity
+
+F32 = mybir.dt.float32
+BF16 = mybir.dt.bfloat16
+U32 = mybir.dt.uint32
+U8 = mybir.dt.uint8
+FP8X4 = mybir.dt.float8_e4m3fn_x4
+ALU = mybir.AluOpType
+ACT = mybir.ActivationFunctionType
+
+P = 128
+M = 5
+B = 2048
+H = 512
+O = 64
+O2 = 128
+CH = 512
+NCH = B // CH
+R = CH // P
+EPS = 1e-6
+CLAMP = 14.0
+DELTA = 1.0 / (1.0 + math.exp(CLAMP))
+
+FLOPS = 2 * M * B * H * H + 2 * M * B * H * O2
+
+
+def tile_gaussianmixturemlp_pa_kernel(tc, h1, W2, b2, W3, b3, out_0, out_1):
+    nc = tc.nc
+    with ExitStack() as ctx:
+        const = ctx.enter_context(tc.tile_pool(name="const", bufs=1))
+        keep = ctx.enter_context(tc.tile_pool(name="keep", bufs=1))
+        wraw = ctx.enter_context(tc.tile_pool(name="wraw", bufs=2))
+        xin = ctx.enter_context(tc.tile_pool(name="xin", bufs=4))
+        work = ctx.enter_context(tc.tile_pool(name="work", bufs=3))
+        codes = ctx.enter_context(tc.tile_pool(name="codes", bufs=3))
+        epi = ctx.enter_context(tc.tile_pool(name="epi", bufs=3))
+        ps_tp = ctx.enter_context(tc.psum_pool(name="ps_tp", bufs=2))
+        ps_l1 = ctx.enter_context(tc.psum_pool(name="ps_l1", bufs=4))
+        ps_l2 = ctx.enter_context(tc.psum_pool(name="ps_l2", bufs=2))
+
+        ident = const.tile([P, P], F32)
+        make_identity(nc, ident[:])
+        neg_clamp = const.tile([P, 1], F32)
+        nc.vector.memset(neg_clamp[:], -CLAMP)
+
+        w2c = keep.tile([P, M, H], U32, align_bytes=64)
+        w2s = keep.tile([P, M, H], U8, align_bytes=64)
+        w3c = keep.tile([P, M, O2], U32, align_bytes=64)
+        w3s = keep.tile([P, M, O2], U8, align_bytes=64)
+        q_all = keep.tile([P, NCH, 2, R * O], F32)
+        a2_all = keep.tile([P, NCH, R * O], F32)
+
+        b2raw = const.tile([P, M, 4], BF16)
+        b2f = const.tile([P, M, 4], F32)
+        b3raw = const.tile([P, M, O2], BF16)
+        b3f = const.tile([P, M, O2], F32)
+        b3m = const.tile([P, O], F32)
+
+        def load_biases():
+            nc.scalar.dma_start(out=b2raw[:], in_=b2.rearrange("m (p t) -> p m t", t=4))
+            nc.vector.tensor_copy(out=b2f[:], in_=b2raw[:])
+            nc.scalar.dma_start(
+                out=b3raw[:].rearrange("p m o -> p (m o)"),
+                in_=b3.rearrange("m o -> (m o)").partition_broadcast(P),
+            )
+            nc.vector.tensor_copy(out=b3f[:, :, 0:O], in_=b3raw[:, :, 0:O])
+            nc.vector.tensor_scalar_add(out=b3f[:, :, O:O2], in0=b3raw[:, :, O:O2], scalar1=-CLAMP)
+            nc.vector.tensor_reduce(
+                out=b3m[:],
+                in_=b3f[:, :, 0:O].rearrange("p m o -> p o m"),
+                axis=mybir.AxisListType.X,
+                op=ALU.add,
+            )
+            nc.vector.tensor_scalar_mul(out=b3m[:], in0=b3m[:], scalar1=1.0 / M)
+
+        def words_to_grouped(engine_copy, grouped, first_tile, bank):
+            dst = grouped[:].bitcast(F32).rearrange("q (r c u) -> q r c u", c=P, u=2)
+            engine_copy(
+                out=dst[:, first_tile : first_tile + 2],
+                in_=bank[:].rearrange("q a u c -> q a c u"),
+            )
+
+        def prep_weights(m):
+            w2raw = wraw.tile([P, 4 * H], BF16)
+            nc.sync.dma_start(out=w2raw[:], in_=W2[m].rearrange("(p t) k -> p (t k)", t=4))
+            w3raw = wraw.tile([P, H], BF16)
+            nc.sync.dma_start(out=w3raw[:], in_=W3[m])
+            w2w = w2raw[:].bitcast(F32)
+            gw2 = work.tile([P, 4 * H], BF16, align_bytes=64, tag="gw2", bufs=2)
+            for j in range(2):
+                bank = ps_tp.tile([P, 2, 2, P], F32, tag="tp")
+                for a in range(2):
+                    for u in range(2):
+                        off = (2 * j + a) * 256 + u * P
+                        nc.tensor.transpose(bank[:, a, u, :], w2w[:, off : off + P], ident[:])
+                words_to_grouped(nc.vector.tensor_copy, gw2, 2 * j, bank)
+            nc.vector.quantize_mx(out=w2c[:, m, :].bitcast(FP8X4), scales=w2s[:, m, :], in_=gw2[:])
+
+            w3w = w3raw[:].bitcast(F32).rearrange("o (p u) -> o p u", u=2)
+            gw3 = work.tile([P, 4 * O2], BF16, align_bytes=64, tag="gw3", bufs=2)
+            bank = ps_tp.tile([P, 2, 2, P], F32, tag="tp")
+            for u in range(2):
+                nc.tensor.transpose(bank[:, 0, u, :], w3w[:, :, u], ident[:])
+            nc.vector.tensor_copy(
+                out=gw3[:].bitcast(F32).rearrange("p (o u) -> p o u", u=2),
+                in_=bank[:, 0].rearrange("p u o -> p o u"),
+            )
+            nc.vector.quantize_mx(out=w3c[:, m, :].bitcast(FP8X4), scales=w3s[:, m, :], in_=gw3[:])
+
+        for c in range(NCH):
+            c2_list = []
+            acc = epi.tile([P, R, O2], F32, tag="acc", bufs=2)
+            for m in range(M):
+                if c == 0:
+                    prep_weights(m)
+                x = xin.tile([P, R * H], BF16)
+                nc.sync.dma_start(
+                    out=x[:],
+                    in_=h1[m, c * CH : (c + 1) * CH, :].rearrange("(p r) k -> p (r k)", r=R),
+                )
+                if c == 0 and m == 0:
+                    load_biases()
+                xw = x[:].bitcast(F32)
+                g1 = work.tile([P, 4 * CH], BF16, align_bytes=64, tag="g1")
+                for j in range(2):
+                    bank = ps_tp.tile([P, 2, 2, P], F32, tag="tp")
+                    for a in range(2):
+                        for u in range(2):
+                            off = (2 * j + a) * 256 + u * P
+                            nc.tensor.transpose(bank[:, a, u, :], xw[:, off : off + P], ident[:])
+                    words_to_grouped(nc.scalar.copy, g1, 2 * j, bank)
+                c1 = codes.tile([P, CH], U32, align_bytes=64, tag="c1")
+                s1 = codes.tile([P, CH], U8, align_bytes=64, tag="s1")
+                nc.vector.quantize_mx(out=c1[:].bitcast(FP8X4), scales=s1[:], in_=g1[:])
+
+                planes = work.tile([P, 4, CH], BF16, tag="planes")
+                for t in range(4):
+                    acc1 = ps_l1.tile([P, CH], F32, tag="l1")
+                    nc.tensor.matmul_mx(
+                        out=acc1[:],
+                        lhsT=w2c[:, m, t * P : (t + 1) * P].bitcast(FP8X4),
+                        lhsT_scale=w2s[:, m, t * P : (t + 1) * P],
+                        rhs=c1[:].bitcast(FP8X4),
+                        rhs_scale=s1[:],
+                        start=True,
+                        stop=True,
+                    )
+                    nc.scalar.activation(
+                        out=planes[:, t, :],
+                        in_=acc1[:],
+                        func=ACT.Relu,
+                        bias=b2f[:, m, t : t + 1],
+                        scale=1.0,
+                    )
+                g2 = work.tile([P, 4 * CH], BF16, align_bytes=64, tag="g2")
+                nc.vector.tensor_copy(
+                    out=g2[:].rearrange("p (c i t) -> p c t i", i=4, t=4),
+                    in_=planes[:].rearrange("p t (c i) -> p c t i", i=4),
+                )
+                c2 = codes.tile([P, CH], U32, align_bytes=64, tag="c2", bufs=8)
+                s2 = codes.tile([P, CH], U8, align_bytes=64, tag="s2", bufs=8)
+                nc.vector.quantize_mx(out=c2[:].bitcast(FP8X4), scales=s2[:], in_=g2[:])
+                c2_list.append((c2, s2))
+
+                yb = ps_l2.tile([P, R, O2], F32, tag="l2")
+                for r in range(R):
+                    nc.tensor.matmul_mx(
+                        out=yb[:, r, :],
+                        lhsT=c2[:, r * P : (r + 1) * P].bitcast(FP8X4),
+                        lhsT_scale=s2[:, r * P : (r + 1) * P],
+                        rhs=w3c[:, m, :].bitcast(FP8X4),
+                        rhs_scale=w3s[:, m, :],
+                        start=True,
+                        stop=True,
+                    )
+                y = epi.tile([P, R, O2], F32, tag="y")
+                nc.vector.tensor_tensor(
+                    out=y[:],
+                    in0=yb[:],
+                    in1=b3f[:, m, :].unsqueeze(1).to_broadcast([P, R, O2]),
+                    op=ALU.add,
+                )
+                sg = epi.tile([P, R, O], F32, tag="sg")
+                nc.scalar.activation(
+                    out=sg[:], in_=y[:, :, O:O2], func=ACT.Sigmoid, bias=neg_clamp[:], scale=-1.0
+                )
+                nc.scalar.activation(out=y[:, :, 0:O], in_=y[:, :, 0:O], func=ACT.Square)
+                half = 0 if m < 3 else 1
+                q = q_all[:, c, half, :]
+                sgf = sg[:].rearrange("p r o -> p (r o)")
+                if m == 0 or m == 3:
+                    nc.vector.tensor_scalar_max(out=q, in0=sgf, scalar1=DELTA)
+                else:
+                    nc.vector.scalar_tensor_tensor(
+                        out=q, in0=sgf, scalar=DELTA, in1=q, op0=ALU.max, op1=ALU.mult
+                    )
+                yf = y[:].rearrange("p r o -> p (r o)")
+                accf = acc[:].rearrange("p r o -> p (r o)")
+                if m == 0:
+                    nc.vector.tensor_scalar(
+                        out=accf, in0=yf, scalar1=0.0, scalar2=0.5 * M * EPS, op0=ALU.max, op1=ALU.add
+                    )
+                else:
+                    nc.vector.scalar_tensor_tensor(
+                        out=accf, in0=yf, scalar=0.0, in1=accf, op0=ALU.max, op1=ALU.add
+                    )
+
+            tb = ps_l2.tile([P, R, O2], F32, tag="l2")
+            for r in range(R):
+                for m in range(M):
+                    c2, s2 = c2_list[m]
+                    nc.tensor.matmul_mx(
+                        out=tb[:, r, :],
+                        lhsT=c2[:, r * P : (r + 1) * P].bitcast(FP8X4),
+                        lhsT_scale=s2[:, r * P : (r + 1) * P],
+                        rhs=w3c[:, m, :].bitcast(FP8X4),
+                        rhs_scale=w3s[:, m, :],
+                        start=(m == 0),
+                        stop=(m == M - 1),
+                    )
+            mean = epi.tile([P, R, O], F32, tag="mean", bufs=2)
+            nc.vector.scalar_tensor_tensor(
+                out=mean[:],
+                in0=tb[:, :, 0:O],
+                scalar=1.0 / M,
+                in1=b3m[:].unsqueeze(1).to_broadcast([P, R, O]),
+                op0=ALU.mult,
+                op1=ALU.add,
+            )
+            nc.sync.dma_start(
+                out=out_0[c * CH : (c + 1) * CH, :].rearrange("(p r) o -> p (r o)", r=R),
+                in_=mean[:].rearrange("p r o -> p (r o)"),
+            )
+            msq = epi.tile([P, R, O], F32, tag="msq", bufs=2)
+            nc.scalar.activation(out=msq[:], in_=mean[:], func=ACT.Square)
+            a1 = epi.tile([P, R, O], F32, tag="a1", bufs=2)
+            nc.vector.tensor_tensor(out=a1[:], in0=acc[:, :, 0:O], in1=acc[:, :, O:O2], op=ALU.add)
+            nc.vector.scalar_tensor_tensor(
+                out=a2_all[:, c, :],
+                in0=a1[:].rearrange("p r o -> p (r o)"),
+                scalar=1.0 / M,
+                in1=msq[:].rearrange("p r o -> p (r o)"),
+                op0=ALU.mult,
+                op1=ALU.subtract,
+            )
+
+        lnq = keep.tile([P, NCH, 2, R * O], F32)
+        nc.scalar.activation(out=lnq[:], in_=q_all[:], func=ACT.Ln)
+        for c in range(NCH):
+            var = epi.tile([P, R * O], F32, tag="var", bufs=2)
+            nc.vector.scalar_tensor_tensor(
+                out=var[:], in0=lnq[:, c, 0, :], scalar=-1.0 / M, in1=a2_all[:, c, :], op0=ALU.mult, op1=ALU.add
+            )
+            nc.vector.scalar_tensor_tensor(
+                out=var[:], in0=lnq[:, c, 1, :], scalar=-1.0 / M, in1=var[:], op0=ALU.mult, op1=ALU.add
+            )
+            nc.vector.tensor_scalar(
+                out=var[:], in0=var[:], scalar1=0.0, scalar2=EPS, op0=ALU.max, op1=ALU.add
+            )
+            nc.sync.dma_start(
+                out=out_1[c * CH : (c + 1) * CH, :].rearrange("(p r) o -> p (r o)", r=R), in_=var[:]
+            )

@@ -1,9 +1,7 @@
 import math
 from contextlib import ExitStack
 
-import concourse.bass as bass
 import concourse.mybir as mybir
-import concourse.tile as tile
 from concourse.masks import make_identity
 
 F32 = mybir.dt.float32
@@ -23,11 +21,15 @@ O2 = 128
 CH = 512
 NCH = B // CH
 R = CH // P
+NU = NCH * M
 EPS = 1e-6
 CLAMP = 14.0
 DELTA = 1.0 / (1.0 + math.exp(CLAMP))
+LN_SCALE = 2.0 ** 40
 
 FLOPS = 2 * M * B * H * H + 2 * M * B * H * O2
+
+W_JOBS = {-2: [0, 1], -1: [2, 3], 0: [4]}
 
 
 def tile_gaussianmixturemlp_pa_kernel(tc, h1, W2, b2, W3, b3, out_0, out_1):
@@ -35,40 +37,59 @@ def tile_gaussianmixturemlp_pa_kernel(tc, h1, W2, b2, W3, b3, out_0, out_1):
     with ExitStack() as ctx:
         const = ctx.enter_context(tc.tile_pool(name="const", bufs=1))
         keep = ctx.enter_context(tc.tile_pool(name="keep", bufs=1))
-        wraw = ctx.enter_context(tc.tile_pool(name="wraw", bufs=2))
-        xin = ctx.enter_context(tc.tile_pool(name="xin", bufs=4))
+        wraw = ctx.enter_context(tc.tile_pool(name="wraw", bufs=M))
+        xin = ctx.enter_context(tc.tile_pool(name="xin", bufs=5))
         work = ctx.enter_context(tc.tile_pool(name="work", bufs=3))
         codes = ctx.enter_context(tc.tile_pool(name="codes", bufs=3))
         epi = ctx.enter_context(tc.tile_pool(name="epi", bufs=3))
-        ps_tp = ctx.enter_context(tc.psum_pool(name="ps_tp", bufs=2))
-        ps_l1 = ctx.enter_context(tc.psum_pool(name="ps_l1", bufs=4))
-        ps_l2 = ctx.enter_context(tc.psum_pool(name="ps_l2", bufs=2))
+        psum = ctx.enter_context(tc.psum_pool(name="psum", bufs=8))
+        ctx.enter_context(tc.manual_schedule())
 
         ident = const.tile([P, P], F32)
-        make_identity(nc, ident[:])
         neg_clamp = const.tile([P, 1], F32)
-        nc.vector.memset(neg_clamp[:], -CLAMP)
-
-        w2c = keep.tile([P, M, H], U32, align_bytes=64)
-        w2s = keep.tile([P, M, H], U8, align_bytes=64)
-        w3c = keep.tile([P, M, O2], U32, align_bytes=64)
-        w3s = keep.tile([P, M, O2], U8, align_bytes=64)
-        q_all = keep.tile([P, NCH, 2, R * O], F32)
-        a2_all = keep.tile([P, NCH, R * O], F32)
-
+        ones = const.tile([P, 1], F32)
+        ln_shift = const.tile([P, 1], F32)
+        acc_init = const.tile([P, 1], F32)
         b2raw = const.tile([P, M, 4], BF16)
         b2f = const.tile([P, M, 4], F32)
         b3raw = const.tile([P, M, O2], BF16)
         b3f = const.tile([P, M, O2], F32)
         b3m = const.tile([P, O], F32)
 
-        def load_biases():
+        w2c = keep.tile([P, M, H], U32, align_bytes=64)
+        w2s = keep.tile([P, M, H], U8, align_bytes=64)
+        w3c = keep.tile([P, M, O2], U32, align_bytes=64)
+        w3s = keep.tile([P, M, O2], U8, align_bytes=64)
+        q_all = keep.tile([P, NCH, R * O], F32)
+        a2_all = keep.tile([P, NCH, R * O], F32)
+        lnq = keep.tile([P, NCH, R * O], F32)
+        var = keep.tile([P, NCH, R * O], F32)
+
+        unit = {}
+        wt = {}
+        chunk = {}
+
+        def valid(u):
+            return 0 <= u < NU
+
+        def setup():
+            make_identity(nc, ident[:])
+            nc.vector.memset(neg_clamp[:], -CLAMP)
+            nc.vector.memset(ones[:], 1.0)
             nc.scalar.dma_start(out=b2raw[:], in_=b2.rearrange("m (p t) -> p m t", t=4))
-            nc.vector.tensor_copy(out=b2f[:], in_=b2raw[:])
             nc.scalar.dma_start(
                 out=b3raw[:].rearrange("p m o -> p (m o)"),
                 in_=b3.rearrange("m o -> (m o)").partition_broadcast(P),
             )
+            nc.scalar.activation(out=ln_shift[:], in_=ones[:], func=ACT.Ln, scale=LN_SCALE)
+            nc.vector.tensor_scalar(
+                out=acc_init[:], in0=ln_shift[:], scalar1=0.5, scalar2=0.5 * M * EPS, op0=ALU.mult, op1=ALU.add
+            )
+
+        def bias2():
+            nc.vector.tensor_copy(out=b2f[:], in_=b2raw[:])
+
+        def bias3():
             nc.vector.tensor_copy(out=b3f[:, :, 0:O], in_=b3raw[:, :, 0:O])
             nc.vector.tensor_scalar_add(out=b3f[:, :, O:O2], in0=b3raw[:, :, O:O2], scalar1=-CLAMP)
             nc.vector.tensor_reduce(
@@ -79,155 +100,213 @@ def tile_gaussianmixturemlp_pa_kernel(tc, h1, W2, b2, W3, b3, out_0, out_1):
             )
             nc.vector.tensor_scalar_mul(out=b3m[:], in0=b3m[:], scalar1=1.0 / M)
 
-        def words_to_grouped(engine_copy, grouped, first_tile, bank):
-            dst = grouped[:].bitcast(F32).rearrange("q (r c u) -> q r c u", c=P, u=2)
-            engine_copy(
-                out=dst[:, first_tile : first_tile + 2],
-                in_=bank[:].rearrange("q a u c -> q a c u"),
-            )
-
-        def prep_weights(m):
-            w2raw = wraw.tile([P, 4 * H], BF16)
+        def load_w(m):
+            w2raw = wraw.tile([P, 4 * H], BF16, tag="w2raw")
             nc.sync.dma_start(out=w2raw[:], in_=W2[m].rearrange("(p t) k -> p (t k)", t=4))
-            w3raw = wraw.tile([P, H], BF16)
+            w3raw = wraw.tile([P, H], BF16, tag="w3raw")
             nc.sync.dma_start(out=w3raw[:], in_=W3[m])
-            w2w = w2raw[:].bitcast(F32)
-            gw2 = work.tile([P, 4 * H], BF16, align_bytes=64, tag="gw2", bufs=2)
-            for j in range(2):
-                bank = ps_tp.tile([P, 2, 2, P], F32, tag="tp")
-                for a in range(2):
-                    for u in range(2):
-                        off = (2 * j + a) * 256 + u * P
-                        nc.tensor.transpose(bank[:, a, u, :], w2w[:, off : off + P], ident[:])
-                words_to_grouped(nc.vector.tensor_copy, gw2, 2 * j, bank)
-            nc.vector.quantize_mx(out=w2c[:, m, :].bitcast(FP8X4), scales=w2s[:, m, :], in_=gw2[:])
+            wt[m] = {"w2raw": w2raw, "w3raw": w3raw}
 
-            w3w = w3raw[:].bitcast(F32).rearrange("o (p u) -> o p u", u=2)
-            gw3 = work.tile([P, 4 * O2], BF16, align_bytes=64, tag="gw3", bufs=2)
-            bank = ps_tp.tile([P, 2, 2, P], F32, tag="tp")
-            for u in range(2):
-                nc.tensor.transpose(bank[:, 0, u, :], w3w[:, :, u], ident[:])
-            nc.vector.tensor_copy(
-                out=gw3[:].bitcast(F32).rearrange("p (o u) -> p o u", u=2),
-                in_=bank[:, 0].rearrange("p u o -> p o u"),
+        def load_x(u):
+            if not valid(u):
+                return
+            c, m = divmod(u, M)
+            x = xin.tile([P, R * H], BF16, tag="x")
+            nc.sync.dma_start(
+                out=x[:], in_=h1[m, c * CH : (c + 1) * CH, :].rearrange("(p r) k -> p (r k)", r=R)
             )
-            nc.vector.quantize_mx(out=w3c[:, m, :].bitcast(FP8X4), scales=w3s[:, m, :], in_=gw3[:])
+            unit[u] = {"x": x}
 
-        for c in range(NCH):
-            c2_list = []
-            acc = epi.tile([P, R, O2], F32, tag="acc", bufs=2)
-            for m in range(M):
-                if c == 0:
-                    prep_weights(m)
-                x = xin.tile([P, R * H], BF16)
-                nc.sync.dma_start(
-                    out=x[:],
-                    in_=h1[m, c * CH : (c + 1) * CH, :].rearrange("(p r) k -> p (r k)", r=R),
-                )
-                if c == 0 and m == 0:
-                    load_biases()
-                xw = x[:].bitcast(F32)
-                g1 = work.tile([P, 4 * CH], BF16, align_bytes=64, tag="g1")
-                for j in range(2):
-                    bank = ps_tp.tile([P, 2, 2, P], F32, tag="tp")
-                    for a in range(2):
-                        for u in range(2):
-                            off = (2 * j + a) * 256 + u * P
-                            nc.tensor.transpose(bank[:, a, u, :], xw[:, off : off + P], ident[:])
-                    words_to_grouped(nc.scalar.copy, g1, 2 * j, bank)
-                c1 = codes.tile([P, CH], U32, align_bytes=64, tag="c1")
-                s1 = codes.tile([P, CH], U8, align_bytes=64, tag="s1")
-                nc.vector.quantize_mx(out=c1[:].bitcast(FP8X4), scales=s1[:], in_=g1[:])
+        def transpose_pair(src_words, j):
+            bank = psum.tile([P, 2, 2, P], F32, tag="bank")
+            for a in range(2):
+                for w in range(2):
+                    off = (2 * j + a) * 256 + w * P
+                    nc.tensor.transpose(bank[:, a, w, :], src_words[:, off : off + P], ident[:])
+            return bank
 
-                planes = work.tile([P, 4, CH], BF16, tag="planes")
-                for t in range(4):
-                    acc1 = ps_l1.tile([P, CH], F32, tag="l1")
-                    nc.tensor.matmul_mx(
-                        out=acc1[:],
-                        lhsT=w2c[:, m, t * P : (t + 1) * P].bitcast(FP8X4),
-                        lhsT_scale=w2s[:, m, t * P : (t + 1) * P],
-                        rhs=c1[:].bitcast(FP8X4),
-                        rhs_scale=s1[:],
-                        start=True,
-                        stop=True,
-                    )
-                    nc.scalar.activation(
-                        out=planes[:, t, :],
-                        in_=acc1[:],
-                        func=ACT.Relu,
-                        bias=b2f[:, m, t : t + 1],
-                        scale=1.0,
-                    )
-                g2 = work.tile([P, 4 * CH], BF16, align_bytes=64, tag="g2")
-                nc.vector.tensor_copy(
-                    out=g2[:].rearrange("p (c i t) -> p c t i", i=4, t=4),
-                    in_=planes[:].rearrange("p t (c i) -> p c t i", i=4),
-                )
-                c2 = codes.tile([P, CH], U32, align_bytes=64, tag="c2", bufs=8)
-                s2 = codes.tile([P, CH], U8, align_bytes=64, tag="s2", bufs=8)
-                nc.vector.quantize_mx(out=c2[:].bitcast(FP8X4), scales=s2[:], in_=g2[:])
-                c2_list.append((c2, s2))
+        def words_out(copy, grouped, j, bank):
+            dst = grouped[:].bitcast(F32).rearrange("q (r c w) -> q r c w", c=P, w=2)
+            copy(out=dst[:, 2 * j : 2 * j + 2], in_=bank[:].rearrange("q a w c -> q a c w"))
 
-                yb = ps_l2.tile([P, R, O2], F32, tag="l2")
-                for r in range(R):
-                    nc.tensor.matmul_mx(
-                        out=yb[:, r, :],
-                        lhsT=c2[:, r * P : (r + 1) * P].bitcast(FP8X4),
-                        lhsT_scale=s2[:, r * P : (r + 1) * P],
-                        rhs=w3c[:, m, :].bitcast(FP8X4),
-                        rhs_scale=w3s[:, m, :],
-                        start=True,
-                        stop=True,
-                    )
-                y = epi.tile([P, R, O2], F32, tag="y")
-                nc.vector.tensor_tensor(
-                    out=y[:],
-                    in0=yb[:],
-                    in1=b3f[:, m, :].unsqueeze(1).to_broadcast([P, R, O2]),
-                    op=ALU.add,
-                )
-                sg = epi.tile([P, R, O], F32, tag="sg")
-                nc.scalar.activation(
-                    out=sg[:], in_=y[:, :, O:O2], func=ACT.Sigmoid, bias=neg_clamp[:], scale=-1.0
-                )
-                nc.scalar.activation(out=y[:, :, 0:O], in_=y[:, :, 0:O], func=ACT.Square)
-                half = 0 if m < 3 else 1
-                q = q_all[:, c, half, :]
-                sgf = sg[:].rearrange("p r o -> p (r o)")
-                if m == 0 or m == 3:
-                    nc.vector.tensor_scalar_max(out=q, in0=sgf, scalar1=DELTA)
-                else:
-                    nc.vector.scalar_tensor_tensor(
-                        out=q, in0=sgf, scalar=DELTA, in1=q, op0=ALU.max, op1=ALU.mult
-                    )
-                yf = y[:].rearrange("p r o -> p (r o)")
-                accf = acc[:].rearrange("p r o -> p (r o)")
-                if m == 0:
-                    nc.vector.tensor_scalar(
-                        out=accf, in0=yf, scalar1=0.0, scalar2=0.5 * M * EPS, op0=ALU.max, op1=ALU.add
-                    )
-                else:
-                    nc.vector.scalar_tensor_tensor(
-                        out=accf, in0=yf, scalar=0.0, in1=accf, op0=ALU.max, op1=ALU.add
-                    )
+        def w_prepare(m):
+            d = wt[m]
+            gw2 = work.tile([P, 4 * H], BF16, align_bytes=64, tag="gw2", bufs=2)
+            gw3 = work.tile([P, 4 * O2], BF16, align_bytes=64, tag="gw3", bufs=2)
+            for j in range(2):
+                bank = transpose_pair(d["w2raw"][:].bitcast(F32), j)
+                words_out(nc.scalar.copy, gw2, j, bank)
+            w3w = d["w3raw"][:].bitcast(F32).rearrange("o (p w) -> o p w", w=2)
+            bank3 = psum.tile([P, 2, 2, P], F32, tag="bank")
+            for w in range(2):
+                nc.tensor.transpose(bank3[:, 0, w, :], w3w[:, :, w], ident[:])
+            nc.vector.tensor_copy(
+                out=gw3[:].bitcast(F32).rearrange("p (o w) -> p o w", w=2),
+                in_=bank3[:, 0].rearrange("p w o -> p o w"),
+            )
+            d["gw2"] = gw2
+            d["gw3"] = gw3
 
-            tb = ps_l2.tile([P, R, O2], F32, tag="l2")
+        def w_quantise(m):
+            d = wt[m]
+            nc.vector.quantize_mx(out=w2c[:, m, :].bitcast(FP8X4), scales=w2s[:, m, :], in_=d["gw2"][:])
+            nc.vector.quantize_mx(out=w3c[:, m, :].bitcast(FP8X4), scales=w3s[:, m, :], in_=d["gw3"][:])
+
+        def x_transposes(u, j):
+            if valid(u):
+                unit[u]["tp%d" % j] = transpose_pair(unit[u]["x"][:].bitcast(F32), j)
+
+        def x_exit(u, j):
+            if not valid(u):
+                return
+            d = unit[u]
+            if j == 0:
+                d["g1"] = work.tile([P, 4 * CH], BF16, align_bytes=64, tag="g1", name="g1")
+            words_out(nc.scalar.copy, d["g1"], j, d["tp%d" % j])
+
+        def quantise1(u):
+            if not valid(u):
+                return
+            d = unit[u]
+            c1 = codes.tile([P, CH], U32, align_bytes=64, tag="c1")
+            s1 = codes.tile([P, CH], U8, align_bytes=64, tag="s1")
+            nc.vector.quantize_mx(out=c1[:].bitcast(FP8X4), scales=s1[:], in_=d["g1"][:])
+            d["c1"] = c1
+            d["s1"] = s1
+
+        def layer1(u, t):
+            if not valid(u):
+                return
+            d = unit[u]
+            m = u % M
+            acc1 = psum.tile([P, CH], F32, tag="bank")
+            nc.tensor.matmul_mx(
+                out=acc1[:],
+                lhsT=w2c[:, m, t * P : (t + 1) * P].bitcast(FP8X4),
+                lhsT_scale=w2s[:, m, t * P : (t + 1) * P],
+                rhs=d["c1"][:].bitcast(FP8X4),
+                rhs_scale=d["s1"][:],
+                start=True,
+                stop=True,
+            )
+            d["l1_%d" % t] = acc1
+
+        def h2_exit(u, t):
+            if not valid(u):
+                return
+            d = unit[u]
+            m = u % M
+            if t == 0:
+                d["planes"] = work.tile([P, 4, CH], BF16, tag="planes", name="planes")
+            nc.scalar.activation(
+                out=d["planes"][:, t, :],
+                in_=d["l1_%d" % t][:],
+                func=ACT.Relu,
+                bias=b2f[:, m, t : t + 1],
+                scale=1.0,
+            )
+
+        def regroup(u):
+            if not valid(u):
+                return
+            d = unit[u]
+            g2 = work.tile([P, 4 * CH], BF16, align_bytes=64, tag="g2")
+            nc.vector.tensor_copy(
+                out=g2[:].rearrange("p (c i t) -> p c t i", i=4, t=4),
+                in_=d["planes"][:].rearrange("p t (c i) -> p c t i", i=4),
+            )
+            d["g2"] = g2
+
+        def quantise2(u):
+            if not valid(u):
+                return
+            d = unit[u]
+            c2 = codes.tile([P, CH], U32, align_bytes=64, tag="c2", bufs=8)
+            s2 = codes.tile([P, CH], U8, align_bytes=64, tag="s2", bufs=8)
+            nc.vector.quantize_mx(out=c2[:].bitcast(FP8X4), scales=s2[:], in_=d["g2"][:])
+            d["c2"] = c2
+            d["s2"] = s2
+
+        def layer2_pass(out, u, r, start, stop):
+            d = unit[u]
+            m = u % M
+            nc.tensor.matmul_mx(
+                out=out,
+                lhsT=d["c2"][:, r * P : (r + 1) * P].bitcast(FP8X4),
+                lhsT_scale=d["s2"][:, r * P : (r + 1) * P],
+                rhs=w3c[:, m, :].bitcast(FP8X4),
+                rhs_scale=w3s[:, m, :],
+                start=start,
+                stop=stop,
+            )
+
+        def layer2(u):
+            if not valid(u):
+                return
+            yb = psum.tile([P, R, O2], F32, tag="bank")
             for r in range(R):
-                for m in range(M):
-                    c2, s2 = c2_list[m]
-                    nc.tensor.matmul_mx(
-                        out=tb[:, r, :],
-                        lhsT=c2[:, r * P : (r + 1) * P].bitcast(FP8X4),
-                        lhsT_scale=s2[:, r * P : (r + 1) * P],
-                        rhs=w3c[:, m, :].bitcast(FP8X4),
-                        rhs_scale=w3s[:, m, :],
-                        start=(m == 0),
-                        stop=(m == M - 1),
-                    )
+                layer2_pass(yb[:, r, :], u, r, True, True)
+            unit[u]["yb"] = yb
+            if u % M == M - 1:
+                c = u // M
+                tb = psum.tile([P, R, O2], F32, tag="bank")
+                for r in range(R):
+                    for m in range(M):
+                        layer2_pass(tb[:, r, :], c * M + m, r, m == 0, m == M - 1)
+                chunk[c]["tb"] = tb
+
+        def add_bias3(u):
+            if not valid(u):
+                return
+            d = unit[u]
+            m = u % M
+            y = epi.tile([P, R, O2], F32, tag="y")
+            nc.vector.tensor_tensor(
+                out=y[:],
+                in0=d["yb"][:],
+                in1=b3f[:, m, :].unsqueeze(1).to_broadcast([P, R, O2]),
+                op=ALU.add,
+            )
+            d["y"] = y
+
+        def nonlinear(u):
+            if not valid(u):
+                return
+            d = unit[u]
+            y = d["y"]
+            sg = epi.tile([P, R, O], F32, tag="sg")
+            nc.scalar.activation(
+                out=sg[:], in_=y[:, :, O:O2], func=ACT.Sigmoid, bias=neg_clamp[:], scale=-1.0
+            )
+            nc.scalar.activation(out=y[:, :, 0:O], in_=y[:, :, 0:O], func=ACT.Square)
+            d["sg"] = sg
+
+        def accumulate(u):
+            if not valid(u):
+                return
+            d = unit[u]
+            c, m = divmod(u, M)
+            if m == 0:
+                chunk[c] = {"acc": epi.tile([P, R, O2], F32, tag="acc", bufs=2, name="acc")}
+            q = q_all[:, c, :]
+            sgf = d["sg"][:].rearrange("p r o -> p (r o)")
+            yf = d["y"][:].rearrange("p r o -> p (r o)")
+            accf = chunk[c]["acc"][:].rearrange("p r o -> p (r o)")
+            if m == 0:
+                nc.vector.tensor_scalar_max(out=q, in0=sgf, scalar1=DELTA)
+                nc.vector.tensor_scalar(
+                    out=accf, in0=yf, scalar1=0.0, scalar2=acc_init[:, 0:1], op0=ALU.max, op1=ALU.add
+                )
+            else:
+                nc.vector.scalar_tensor_tensor(out=q, in0=sgf, scalar=DELTA, in1=q, op0=ALU.max, op1=ALU.mult)
+                nc.vector.scalar_tensor_tensor(out=accf, in0=yf, scalar=0.0, in1=accf, op0=ALU.max, op1=ALU.add)
+
+        def mean_of(c):
+            d = chunk[c]
             mean = epi.tile([P, R, O], F32, tag="mean", bufs=2)
             nc.vector.scalar_tensor_tensor(
                 out=mean[:],
-                in0=tb[:, :, 0:O],
+                in0=d["tb"][:, :, 0:O],
                 scalar=1.0 / M,
                 in1=b3m[:].unsqueeze(1).to_broadcast([P, R, O]),
                 op0=ALU.mult,
@@ -237,32 +316,99 @@ def tile_gaussianmixturemlp_pa_kernel(tc, h1, W2, b2, W3, b3, out_0, out_1):
                 out=out_0[c * CH : (c + 1) * CH, :].rearrange("(p r) o -> p (r o)", r=R),
                 in_=mean[:].rearrange("p r o -> p (r o)"),
             )
+            d["mean"] = mean
+
+        def mean_square(c):
+            d = chunk[c]
             msq = epi.tile([P, R, O], F32, tag="msq", bufs=2)
-            nc.scalar.activation(out=msq[:], in_=mean[:], func=ACT.Square)
+            nc.scalar.activation(out=msq[:], in_=d["mean"][:], func=ACT.Square)
+            d["msq"] = msq
+
+        def spread_of(c):
+            d = chunk[c]
             a1 = epi.tile([P, R, O], F32, tag="a1", bufs=2)
-            nc.vector.tensor_tensor(out=a1[:], in0=acc[:, :, 0:O], in1=acc[:, :, O:O2], op=ALU.add)
+            nc.vector.tensor_tensor(out=a1[:], in0=d["acc"][:, :, 0:O], in1=d["acc"][:, :, O:O2], op=ALU.add)
             nc.vector.scalar_tensor_tensor(
                 out=a2_all[:, c, :],
                 in0=a1[:].rearrange("p r o -> p (r o)"),
                 scalar=1.0 / M,
-                in1=msq[:].rearrange("p r o -> p (r o)"),
+                in1=d["msq"][:].rearrange("p r o -> p (r o)"),
                 op0=ALU.mult,
                 op1=ALU.subtract,
             )
 
-        lnq = keep.tile([P, NCH, 2, R * O], F32)
-        nc.scalar.activation(out=lnq[:], in_=q_all[:], func=ACT.Ln)
-        for c in range(NCH):
-            var = epi.tile([P, R * O], F32, tag="var", bufs=2)
+        def log_of(c0, c1):
+            nc.scalar.activation(out=lnq[:, c0:c1, :], in_=q_all[:, c0:c1, :], func=ACT.Ln, scale=LN_SCALE)
+
+        def variance_of(c0, c1):
+            v = var[:, c0:c1, :].rearrange("p c f -> p (c f)")
             nc.vector.scalar_tensor_tensor(
-                out=var[:], in0=lnq[:, c, 0, :], scalar=-1.0 / M, in1=a2_all[:, c, :], op0=ALU.mult, op1=ALU.add
+                out=v,
+                in0=lnq[:, c0:c1, :].rearrange("p c f -> p (c f)"),
+                scalar=-1.0 / M,
+                in1=a2_all[:, c0:c1, :].rearrange("p c f -> p (c f)"),
+                op0=ALU.mult,
+                op1=ALU.add,
             )
-            nc.vector.scalar_tensor_tensor(
-                out=var[:], in0=lnq[:, c, 1, :], scalar=-1.0 / M, in1=var[:], op0=ALU.mult, op1=ALU.add
-            )
-            nc.vector.tensor_scalar(
-                out=var[:], in0=var[:], scalar1=0.0, scalar2=EPS, op0=ALU.max, op1=ALU.add
-            )
-            nc.sync.dma_start(
-                out=out_1[c * CH : (c + 1) * CH, :].rearrange("(p r) o -> p (r o)", r=R), in_=var[:]
-            )
+            nc.vector.tensor_scalar(out=v, in0=v, scalar1=0.0, scalar2=EPS, op0=ALU.max, op1=ALU.add)
+            for c in range(c0, c1):
+                nc.sync.dma_start(
+                    out=out_1[c * CH : (c + 1) * CH, :].rearrange("(p r) o -> p (r o)", r=R), in_=var[:, c, :]
+                )
+
+        load_w(0)
+        load_x(0)
+        setup()
+        load_w(1)
+        load_x(1)
+        load_w(2)
+        load_w(3)
+        load_x(2)
+        load_w(4)
+        load_x(3)
+        for i in range(-2, NU + 2):
+            if i >= -1:
+                load_x(i + 5)
+            jobs = W_JOBS.get(i, [])
+            done = (i - 2) // M if (valid(i - 2) and (i - 2) % M == M - 1) else -1
+            add_bias3(i - 2)
+            x_exit(i + 1, 0)
+            x_exit(i + 1, 1)
+            if i == -2:
+                w_prepare(jobs[0])
+            x_transposes(i + 2, 0)
+            x_transposes(i + 2, 1)
+            regroup(i - 1)
+            quantise1(i + 1)
+            if done >= 0:
+                mean_of(done)
+            for m in jobs:
+                if i != -2 or m != jobs[0]:
+                    w_prepare(m)
+            h2_exit(i, 0)
+            for m in jobs:
+                w_quantise(m)
+            if i == -2:
+                bias2()
+            if i == 0:
+                bias3()
+            nonlinear(i - 2)
+            if done >= 0:
+                mean_square(done)
+            layer1(i + 1, 0)
+            h2_exit(i, 1)
+            layer1(i + 1, 1)
+            quantise2(i - 1)
+            layer2(i - 1)
+            accumulate(i - 2)
+            if done >= 0:
+                if done == NCH - 1:
+                    log_of(0, NCH - 1)
+                spread_of(done)
+            h2_exit(i, 2)
+            layer1(i + 1, 2)
+            h2_exit(i, 3)
+            layer1(i + 1, 3)
+        log_of(NCH - 1, NCH)
+        variance_of(0, NCH - 1)
+        variance_of(NCH - 1, NCH)

@@ -240,13 +240,28 @@ def tile_gaussianmixturemlp_pa_kernel(tc, h1, W2, b2, W3, b3, out_0, out_1):
                 stop=stop,
             )
 
-        def layer2(u):
+        def hold_clock(u):
             if not valid(u):
                 return
             yb = psum.tile([P, R, O2], F32, tag="bank")
+            for k in range(2):
+                nc.tensor.matmul_mx(
+                    out=yb[:].rearrange("p r o -> p (r o)"),
+                    lhsT=w2c[:, 0, 0:P].bitcast(FP8X4),
+                    lhsT_scale=w2s[:, 0, 0:P],
+                    rhs=w2c[:, 0, :].bitcast(FP8X4),
+                    rhs_scale=w2s[:, 0, :],
+                    start=True,
+                    stop=True,
+                )
+            unit[u]["yb"] = yb
+
+        def layer2(u):
+            if not valid(u):
+                return
+            yb = unit[u]["yb"]
             for r in range(R):
                 layer2_pass(yb[:, r, :], u, r, True, True)
-            unit[u]["yb"] = yb
             if u % M == M - 1:
                 c = u // M
                 tb = psum.tile([P, R, O2], F32, tag="bank")
@@ -378,6 +393,7 @@ def tile_gaussianmixturemlp_pa_kernel(tc, h1, W2, b2, W3, b3, out_0, out_1):
                 w_prepare(jobs[0])
             x_transposes(i + 2, 0)
             x_transposes(i + 2, 1)
+            hold_clock(i - 1)
             regroup(i - 1)
             quantise1(i + 1)
             if done >= 0:

@@ -55,6 +55,7 @@ def tile_gaussianmixturemlp_pa_kernel(tc, h1, W2, b2, W3, b3, out_0, out_1):
         b3raw = const.tile([P, M, O2], BF16)
         b3f = const.tile([P, M, O2], F32)
         b3m = const.tile([P, O], F32)
+        zeros = const.tile([P, CH], BF16)
 
         w2c = keep.tile([P, M, H], U32, align_bytes=64)
         w2s = keep.tile([P, M, H], U8, align_bytes=64)
@@ -72,15 +73,24 @@ def tile_gaussianmixturemlp_pa_kernel(tc, h1, W2, b2, W3, b3, out_0, out_1):
         def valid(u):
             return 0 <= u < NU
 
+        def idle_plain(n):
+            scratch = psum.tile([P, CH], F32, tag="bank")
+            for k in range(n):
+                nc.tensor.matmul(out=scratch[:], lhsT=zeros[:, 0:P], rhs=zeros[:], start=True, stop=True)
+
+        def load_bias3():
+            nc.sync.dma_start(
+                out=b3raw[:].rearrange("p m o -> p (m o)"),
+                in_=b3.rearrange("m o -> (m o)").partition_broadcast(P),
+            )
+
         def setup():
+            nc.vector.memset(zeros[:], 0.0)
+            idle_plain(4)
             make_identity(nc, ident[:])
             nc.vector.memset(neg_clamp[:], -CLAMP)
             nc.vector.memset(ones[:], 1.0)
             nc.scalar.dma_start(out=b2raw[:], in_=b2.rearrange("m (p t) -> p m t", t=4))
-            nc.scalar.dma_start(
-                out=b3raw[:].rearrange("p m o -> p (m o)"),
-                in_=b3.rearrange("m o -> (m o)").partition_broadcast(P),
-            )
             nc.scalar.activation(out=ln_shift[:], in_=ones[:], func=ACT.Ln, scale=LN_SCALE)
             nc.vector.tensor_scalar(
                 out=acc_init[:], in0=ln_shift[:], scalar1=0.5, scalar2=0.5 * M * EPS, op0=ALU.mult, op1=ALU.add
@@ -136,6 +146,7 @@ def tile_gaussianmixturemlp_pa_kernel(tc, h1, W2, b2, W3, b3, out_0, out_1):
             for j in range(2):
                 bank = transpose_pair(d["w2raw"][:].bitcast(F32), j)
                 words_out(nc.scalar.copy, gw2, j, bank)
+            idle_plain(1)
             w3w = d["w3raw"][:].bitcast(F32).rearrange("o (p w) -> o p w", w=2)
             bank3 = psum.tile([P, 2, 2, P], F32, tag="bank")
             for w in range(2):
@@ -240,11 +251,11 @@ def tile_gaussianmixturemlp_pa_kernel(tc, h1, W2, b2, W3, b3, out_0, out_1):
                 stop=stop,
             )
 
-        def hold_clock(u):
+        def hold_clock(u, n):
             if not valid(u):
                 return
             yb = psum.tile([P, R, O2], F32, tag="bank")
-            for k in range(2):
+            for k in range(n):
                 nc.tensor.matmul_mx(
                     out=yb[:].rearrange("p r o -> p (r o)"),
                     lhsT=w2c[:, 0, 0:P].bitcast(FP8X4),
@@ -339,13 +350,17 @@ def tile_gaussianmixturemlp_pa_kernel(tc, h1, W2, b2, W3, b3, out_0, out_1):
             nc.scalar.activation(out=msq[:], in_=d["mean"][:], func=ACT.Square)
             d["msq"] = msq
 
-        def spread_of(c):
+        def spread_sum(c):
             d = chunk[c]
             a1 = epi.tile([P, R, O], F32, tag="a1", bufs=2)
             nc.vector.tensor_tensor(out=a1[:], in0=d["acc"][:, :, 0:O], in1=d["acc"][:, :, O:O2], op=ALU.add)
+            d["a1"] = a1
+
+        def spread_of(c):
+            d = chunk[c]
             nc.vector.scalar_tensor_tensor(
                 out=a2_all[:, c, :],
-                in0=a1[:].rearrange("p r o -> p (r o)"),
+                in0=d["a1"][:].rearrange("p r o -> p (r o)"),
                 scalar=1.0 / M,
                 in1=d["msq"][:].rearrange("p r o -> p (r o)"),
                 op0=ALU.mult,
@@ -381,9 +396,11 @@ def tile_gaussianmixturemlp_pa_kernel(tc, h1, W2, b2, W3, b3, out_0, out_1):
         load_x(2)
         load_w(4)
         load_x(3)
-        for i in range(-2, NU + 2):
+        for i in range(-2, NU):
             if i >= -1:
                 load_x(i + 5)
+            if i == 0:
+                load_bias3()
             jobs = W_JOBS.get(i, [])
             done = (i - 2) // M if (valid(i - 2) and (i - 2) % M == M - 1) else -1
             add_bias3(i - 2)
@@ -393,7 +410,9 @@ def tile_gaussianmixturemlp_pa_kernel(tc, h1, W2, b2, W3, b3, out_0, out_1):
                 w_prepare(jobs[0])
             x_transposes(i + 2, 0)
             x_transposes(i + 2, 1)
-            hold_clock(i - 1)
+            if i < 1:
+                idle_plain(1)
+            hold_clock(i - 1, 2)
             regroup(i - 1)
             quantise1(i + 1)
             if done >= 0:
@@ -406,7 +425,7 @@ def tile_gaussianmixturemlp_pa_kernel(tc, h1, W2, b2, W3, b3, out_0, out_1):
                 w_quantise(m)
             if i == -2:
                 bias2()
-            if i == 0:
+            if i == 1:
                 bias3()
             nonlinear(i - 2)
             if done >= 0:
@@ -418,13 +437,28 @@ def tile_gaussianmixturemlp_pa_kernel(tc, h1, W2, b2, W3, b3, out_0, out_1):
             layer2(i - 1)
             accumulate(i - 2)
             if done >= 0:
-                if done == NCH - 1:
-                    log_of(0, NCH - 1)
+                spread_sum(done)
                 spread_of(done)
             h2_exit(i, 2)
             layer1(i + 1, 2)
             h2_exit(i, 3)
             layer1(i + 1, 3)
+        last = NU - 1
+        hold_clock(last, 3)
+        regroup(last)
+        quantise2(last)
+        add_bias3(last - 1)
+        layer2(last)
+        nonlinear(last - 1)
+        add_bias3(last)
+        nonlinear(last)
+        accumulate(last - 1)
+        log_of(0, NCH - 1)
+        accumulate(last)
+        mean_of(NCH - 1)
+        spread_sum(NCH - 1)
+        mean_square(NCH - 1)
         log_of(NCH - 1, NCH)
         variance_of(0, NCH - 1)
+        spread_of(NCH - 1)
         variance_of(NCH - 1, NCH)

@@ -6,6 +6,7 @@ from concourse.masks import make_identity
 
 F32 = mybir.dt.float32
 BF16 = mybir.dt.bfloat16
+I32 = mybir.dt.int32
 U32 = mybir.dt.uint32
 U8 = mybir.dt.uint8
 FP8X4 = mybir.dt.float8_e4m3fn_x4
@@ -19,6 +20,7 @@ H = 512
 O = 64
 O2 = 128
 CH = 512
+HALF = CH // 2
 NCH = B // CH
 R = CH // P
 NU = NCH * M
@@ -26,10 +28,12 @@ EPS = 1e-6
 CLAMP = 14.0
 DELTA = 1.0 / (1.0 + math.exp(CLAMP))
 LN_SCALE = 2.0 ** 40
+W3W = 5 * O
 
 FLOPS = 2 * M * B * H * H + 2 * M * B * H * O2
 
 W_JOBS = {-2: [0, 1], -1: [2, 3], 0: [4]}
+VECTOR_EXITS = 3
 
 
 def tile_gaussianmixturemlp_pa_kernel(tc, h1, W2, b2, W3, b3, out_0, out_1):
@@ -46,25 +50,28 @@ def tile_gaussianmixturemlp_pa_kernel(tc, h1, W2, b2, W3, b3, out_0, out_1):
         ctx.enter_context(tc.manual_schedule())
 
         ident = const.tile([P, P], F32)
-        neg_clamp = const.tile([P, 1], F32)
+        identb = const.tile([P, P], BF16)
         ones = const.tile([P, 1], F32)
         ln_shift = const.tile([P, 1], F32)
-        acc_init = const.tile([P, 1], F32)
+        zeros = const.tile([P, CH], BF16)
         b2raw = const.tile([P, M, 4], BF16)
         b2f = const.tile([P, M, 4], F32)
-        b3raw = const.tile([P, M, O2], BF16)
-        b3f = const.tile([P, M, O2], F32)
-        b3m = const.tile([P, O], F32)
-        zeros = const.tile([P, CH], BF16)
+        b3rows = const.tile([P, P], BF16)
+        b3col = const.tile([P, M, 2], F32)
+        neg_bv = const.tile([P, M], F32)
+        floor_x = const.tile([P, M], F32)
+        floor_sum = const.tile([P, 1], F32)
+        acc_init = const.tile([P, 1], F32)
+        b_mean = const.tile([P, 1], F32)
 
         w2c = keep.tile([P, M, H], U32, align_bytes=64)
         w2s = keep.tile([P, M, H], U8, align_bytes=64)
-        w3c = keep.tile([P, M, O2], U32, align_bytes=64)
-        w3s = keep.tile([P, M, O2], U8, align_bytes=64)
-        q_all = keep.tile([P, NCH, R * O], F32)
-        a2_all = keep.tile([P, NCH, R * O], F32)
-        lnq = keep.tile([P, NCH, R * O], F32)
-        var = keep.tile([P, NCH, R * O], F32)
+        w3c = keep.tile([P, M, W3W], U32, align_bytes=64)
+        w3s = keep.tile([P, M, W3W], U8, align_bytes=64)
+        q_all = keep.tile([P, NCH, HALF], F32)
+        a2_all = keep.tile([P, NCH, HALF], F32)
+        lnq = keep.tile([P, NCH, HALF], F32)
+        var = keep.tile([P, NCH, HALF], F32)
 
         unit = {}
         wt = {}
@@ -78,37 +85,40 @@ def tile_gaussianmixturemlp_pa_kernel(tc, h1, W2, b2, W3, b3, out_0, out_1):
             for k in range(n):
                 nc.tensor.matmul(out=scratch[:], lhsT=zeros[:, 0:P], rhs=zeros[:], start=True, stop=True)
 
-        def load_bias3():
-            nc.sync.dma_start(
-                out=b3raw[:].rearrange("p m o -> p (m o)"),
-                in_=b3.rearrange("m o -> (m o)").partition_broadcast(P),
-            )
-
         def setup():
             nc.vector.memset(zeros[:], 0.0)
             idle_plain(4)
             make_identity(nc, ident[:])
-            nc.vector.memset(neg_clamp[:], -CLAMP)
+            make_identity(nc, identb[:])
             nc.vector.memset(ones[:], 1.0)
+            nc.vector.memset(b3rows[:], 0.0)
+            nc.vector.memset(w3c[:].bitcast(I32), 0)
+            nc.vector.memset(w3s[:].bitcast(I32), 0)
             nc.scalar.dma_start(out=b2raw[:], in_=b2.rearrange("m (p t) -> p m t", t=4))
+            b3_rows = b3.rearrange("m (k o) -> (m k) o", k=2)
+            nc.scalar.dma_start(out=b3rows[0 : 2 * M, 0:O], in_=b3_rows)
+            nc.scalar.dma_start(out=b3rows[0 : 2 * M, O:O2], in_=b3_rows)
             nc.scalar.activation(out=ln_shift[:], in_=ones[:], func=ACT.Ln, scale=LN_SCALE)
-            nc.vector.tensor_scalar(
-                out=acc_init[:], in0=ln_shift[:], scalar1=0.5, scalar2=0.5 * M * EPS, op0=ALU.mult, op1=ALU.add
-            )
 
         def bias2():
             nc.vector.tensor_copy(out=b2f[:], in_=b2raw[:])
 
+        def bias3_transpose():
+            bank = psum.tile([P, P], BF16, tag="bank")
+            nc.tensor.transpose(bank[:], b3rows[:], identb[:])
+            nc.vector.tensor_copy(out=b3col[:].rearrange("p m k -> p (m k)"), in_=bank[:, 0 : 2 * M])
+
         def bias3():
-            nc.vector.tensor_copy(out=b3f[:, :, 0:O], in_=b3raw[:, :, 0:O])
-            nc.vector.tensor_scalar_add(out=b3f[:, :, O:O2], in0=b3raw[:, :, O:O2], scalar1=-CLAMP)
-            nc.vector.tensor_reduce(
-                out=b3m[:],
-                in_=b3f[:, :, 0:O].rearrange("p m o -> p o m"),
-                axis=mybir.AxisListType.X,
-                op=ALU.add,
+            nc.vector.tensor_scalar_mul(out=neg_bv[:], in0=b3col[:, :, 1], scalar1=-1.0)
+            nc.vector.tensor_scalar(
+                out=floor_x[:], in0=b3col[:, :, 1], scalar1=-1.0, scalar2=CLAMP, op0=ALU.mult, op1=ALU.add
             )
-            nc.vector.tensor_scalar_mul(out=b3m[:], in0=b3m[:], scalar1=1.0 / M)
+            nc.vector.tensor_reduce(out=floor_sum[:], in_=floor_x[:], axis=mybir.AxisListType.X, op=ALU.add)
+            nc.vector.scalar_tensor_tensor(
+                out=acc_init[:], in0=ln_shift[:], scalar=M * EPS, in1=floor_sum[:], op0=ALU.add, op1=ALU.subtract
+            )
+            nc.vector.tensor_reduce(out=b_mean[:], in_=b3col[:, :, 0], axis=mybir.AxisListType.X, op=ALU.add)
+            nc.vector.tensor_scalar_mul(out=b_mean[:], in0=b_mean[:], scalar1=1.0 / M)
 
         def load_w(m):
             w2raw = wraw.tile([P, 4 * H], BF16, tag="w2raw")
@@ -161,7 +171,13 @@ def tile_gaussianmixturemlp_pa_kernel(tc, h1, W2, b2, W3, b3, out_0, out_1):
         def w_quantise(m):
             d = wt[m]
             nc.vector.quantize_mx(out=w2c[:, m, :].bitcast(FP8X4), scales=w2s[:, m, :], in_=d["gw2"][:])
-            nc.vector.quantize_mx(out=w3c[:, m, :].bitcast(FP8X4), scales=w3s[:, m, :], in_=d["gw3"][:])
+            for k in range(2):
+                lo = (2 * k + 1) * O
+                nc.vector.quantize_mx(
+                    out=w3c[:, m, lo : lo + O].bitcast(FP8X4),
+                    scales=w3s[:, m, lo : lo + O],
+                    in_=d["gw3"][:, 4 * O * k : 4 * O * (k + 1)],
+                )
 
         def x_transposes(u, j):
             if valid(u):
@@ -209,13 +225,23 @@ def tile_gaussianmixturemlp_pa_kernel(tc, h1, W2, b2, W3, b3, out_0, out_1):
             m = u % M
             if t == 0:
                 d["planes"] = work.tile([P, 4, CH], BF16, tag="planes", name="planes")
-            nc.scalar.activation(
-                out=d["planes"][:, t, :],
-                in_=d["l1_%d" % t][:],
-                func=ACT.Relu,
-                bias=b2f[:, m, t : t + 1],
-                scale=1.0,
-            )
+            if t == 3 and m < VECTOR_EXITS:
+                nc.vector.tensor_scalar(
+                    out=d["planes"][:, t, :],
+                    in0=d["l1_%d" % t][:],
+                    scalar1=b2f[:, m, t : t + 1],
+                    scalar2=0.0,
+                    op0=ALU.add,
+                    op1=ALU.max,
+                )
+            else:
+                nc.scalar.activation(
+                    out=d["planes"][:, t, :],
+                    in_=d["l1_%d" % t][:],
+                    func=ACT.Relu,
+                    bias=b2f[:, m, t : t + 1],
+                    scale=1.0,
+                )
 
         def regroup(u):
             if not valid(u):
@@ -238,26 +264,28 @@ def tile_gaussianmixturemlp_pa_kernel(tc, h1, W2, b2, W3, b3, out_0, out_1):
             d["c2"] = c2
             d["s2"] = s2
 
-        def layer2_pass(out, u, r, start, stop):
+        def layer2_pair(out, u, k, start, stop):
             d = unit[u]
             m = u % M
-            nc.tensor.matmul_mx(
-                out=out,
-                lhsT=d["c2"][:, r * P : (r + 1) * P].bitcast(FP8X4),
-                lhsT_scale=d["s2"][:, r * P : (r + 1) * P],
-                rhs=w3c[:, m, :].bitcast(FP8X4),
-                rhs_scale=w3s[:, m, :],
-                start=start,
-                stop=stop,
-            )
+            for h in range(2):
+                lo = 2 * O * k + O * (1 - h)
+                nc.tensor.matmul_mx(
+                    out=out,
+                    lhsT=w3c[:, m, lo : lo + P].bitcast(FP8X4),
+                    lhsT_scale=w3s[:, m, lo : lo + P],
+                    rhs=d["c2"][:, h * HALF : (h + 1) * HALF].bitcast(FP8X4),
+                    rhs_scale=d["s2"][:, h * HALF : (h + 1) * HALF],
+                    start=(start and h == 0),
+                    stop=(stop and h == 1),
+                )
 
         def hold_clock(u, n):
             if not valid(u):
                 return
-            yb = psum.tile([P, R, O2], F32, tag="bank")
+            pb = psum.tile([P, 2, HALF], F32, tag="bank")
             for k in range(n):
                 nc.tensor.matmul_mx(
-                    out=yb[:].rearrange("p r o -> p (r o)"),
+                    out=pb[:].rearrange("p k f -> p (k f)"),
                     lhsT=w2c[:, 0, 0:P].bitcast(FP8X4),
                     lhsT_scale=w2s[:, 0, 0:P],
                     rhs=w2c[:, 0, :].bitcast(FP8X4),
@@ -265,46 +293,35 @@ def tile_gaussianmixturemlp_pa_kernel(tc, h1, W2, b2, W3, b3, out_0, out_1):
                     start=True,
                     stop=True,
                 )
-            unit[u]["yb"] = yb
+            unit[u]["pb"] = pb
 
         def layer2(u):
             if not valid(u):
                 return
-            yb = unit[u]["yb"]
-            for r in range(R):
-                layer2_pass(yb[:, r, :], u, r, True, True)
+            d = unit[u]
+            if "pb" not in d:
+                d["pb"] = psum.tile([P, 2, HALF], F32, tag="bank", name="pb")
+            for k in range(2):
+                layer2_pair(d["pb"][:, k, :], u, k, True, True)
             if u % M == M - 1:
                 c = u // M
-                tb = psum.tile([P, R, O2], F32, tag="bank")
-                for r in range(R):
-                    for m in range(M):
-                        layer2_pass(tb[:, r, :], c * M + m, r, m == 0, m == M - 1)
+                tb = psum.tile([P, 2, HALF], F32, tag="bank")
+                for m in range(M):
+                    layer2_pair(tb[:, 0, :], c * M + m, 0, m == 0, m == M - 1)
                 chunk[c]["tb"] = tb
-
-        def add_bias3(u):
-            if not valid(u):
-                return
-            d = unit[u]
-            m = u % M
-            y = epi.tile([P, R, O2], F32, tag="y")
-            nc.vector.tensor_tensor(
-                out=y[:],
-                in0=d["yb"][:],
-                in1=b3f[:, m, :].unsqueeze(1).to_broadcast([P, R, O2]),
-                op=ALU.add,
-            )
-            d["y"] = y
 
         def nonlinear(u):
             if not valid(u):
                 return
             d = unit[u]
-            y = d["y"]
-            sg = epi.tile([P, R, O], F32, tag="sg")
+            m = u % M
+            sq = epi.tile([P, HALF], F32, tag="sq")
+            sg = epi.tile([P, HALF], F32, tag="sg")
+            nc.scalar.activation(out=sq[:], in_=d["pb"][:, 0, :], func=ACT.Square, bias=b3col[:, m, 0:1], scale=1.0)
             nc.scalar.activation(
-                out=sg[:], in_=y[:, :, O:O2], func=ACT.Sigmoid, bias=neg_clamp[:], scale=-1.0
+                out=sg[:], in_=d["pb"][:, 1, :], func=ACT.Sigmoid, bias=neg_bv[:, m : m + 1], scale=-1.0
             )
-            nc.scalar.activation(out=y[:, :, 0:O], in_=y[:, :, 0:O], func=ACT.Square)
+            d["sq"] = sq
             d["sg"] = sg
 
         def accumulate(u):
@@ -313,58 +330,46 @@ def tile_gaussianmixturemlp_pa_kernel(tc, h1, W2, b2, W3, b3, out_0, out_1):
             d = unit[u]
             c, m = divmod(u, M)
             if m == 0:
-                chunk[c] = {"acc": epi.tile([P, R, O2], F32, tag="acc", bufs=2, name="acc")}
+                chunk[c] = {"acc": epi.tile([P, HALF], F32, tag="acc", bufs=2, name="acc")}
             q = q_all[:, c, :]
-            sgf = d["sg"][:].rearrange("p r o -> p (r o)")
-            yf = d["y"][:].rearrange("p r o -> p (r o)")
-            accf = chunk[c]["acc"][:].rearrange("p r o -> p (r o)")
+            acc = chunk[c]["acc"]
+            raw = d["pb"][:, 1, :]
             if m == 0:
-                nc.vector.tensor_scalar_max(out=q, in0=sgf, scalar1=DELTA)
+                nc.vector.tensor_scalar_max(out=q, in0=d["sg"][:], scalar1=DELTA)
                 nc.vector.tensor_scalar(
-                    out=accf, in0=yf, scalar1=0.0, scalar2=acc_init[:, 0:1], op0=ALU.max, op1=ALU.add
+                    out=acc[:], in0=raw, scalar1=floor_x[:, 0:1], scalar2=acc_init[:, 0:1], op0=ALU.max, op1=ALU.add
                 )
             else:
-                nc.vector.scalar_tensor_tensor(out=q, in0=sgf, scalar=DELTA, in1=q, op0=ALU.max, op1=ALU.mult)
-                nc.vector.scalar_tensor_tensor(out=accf, in0=yf, scalar=0.0, in1=accf, op0=ALU.max, op1=ALU.add)
+                nc.vector.scalar_tensor_tensor(out=q, in0=d["sg"][:], scalar=DELTA, in1=q, op0=ALU.max, op1=ALU.mult)
+                nc.vector.scalar_tensor_tensor(
+                    out=acc[:], in0=raw, scalar=floor_x[:, m : m + 1], in1=acc[:], op0=ALU.max, op1=ALU.add
+                )
+            nc.vector.tensor_tensor(out=acc[:], in0=acc[:], in1=d["sq"][:], op=ALU.add)
 
         def mean_of(c):
             d = chunk[c]
-            mean = epi.tile([P, R, O], F32, tag="mean", bufs=2)
-            nc.vector.scalar_tensor_tensor(
-                out=mean[:],
-                in0=d["tb"][:, :, 0:O],
-                scalar=1.0 / M,
-                in1=b3m[:].unsqueeze(1).to_broadcast([P, R, O]),
-                op0=ALU.mult,
-                op1=ALU.add,
-            )
-            nc.sync.dma_start(
-                out=out_0[c * CH : (c + 1) * CH, :].rearrange("(p r) o -> p (r o)", r=R),
-                in_=mean[:].rearrange("p r o -> p (r o)"),
-            )
+            mean = epi.tile([P, HALF], F32, tag="mean", bufs=2)
+            msq = epi.tile([P, HALF], F32, tag="msq", bufs=2)
+            nc.scalar.activation(out=mean[:], in_=d["tb"][:, 0, :], func=ACT.Identity, bias=b_mean[:], scale=1.0 / M)
+            nc.scalar.activation(out=msq[:], in_=d["tb"][:, 0, :], func=ACT.Square, bias=b_mean[:], scale=1.0 / M)
             d["mean"] = mean
-
-        def mean_square(c):
-            d = chunk[c]
-            msq = epi.tile([P, R, O], F32, tag="msq", bufs=2)
-            nc.scalar.activation(out=msq[:], in_=d["mean"][:], func=ACT.Square)
             d["msq"] = msq
-
-        def spread_sum(c):
-            d = chunk[c]
-            a1 = epi.tile([P, R, O], F32, tag="a1", bufs=2)
-            nc.vector.tensor_tensor(out=a1[:], in0=d["acc"][:, :, 0:O], in1=d["acc"][:, :, O:O2], op=ALU.add)
-            d["a1"] = a1
 
         def spread_of(c):
             d = chunk[c]
             nc.vector.scalar_tensor_tensor(
-                out=a2_all[:, c, :],
-                in0=d["a1"][:].rearrange("p r o -> p (r o)"),
-                scalar=1.0 / M,
-                in1=d["msq"][:].rearrange("p r o -> p (r o)"),
-                op0=ALU.mult,
-                op1=ALU.subtract,
+                out=a2_all[:, c, :], in0=d["acc"][:], scalar=1.0 / M, in1=d["msq"][:], op0=ALU.mult, op1=ALU.subtract
+            )
+
+        def write_out(copy, dram, c, src):
+            bank = psum.tile([P, 2, P], F32, tag="bank")
+            for k in range(2):
+                nc.tensor.transpose(bank[:, k, :], src[:, k * P : (k + 1) * P], ident[:])
+            res = epi.tile([P, 2, 2, O], F32, tag="res", bufs=3)
+            copy(out=res[:], in_=bank[:].rearrange("p k (h o) -> p h k o", h=2))
+            nc.sync.dma_start(
+                out=dram[c * CH : (c + 1) * CH, :].rearrange("(p r) o -> p (r o)", r=R),
+                in_=res[:].rearrange("p h k o -> p (h k o)"),
             )
 
         def log_of(c0, c1):
@@ -381,10 +386,6 @@ def tile_gaussianmixturemlp_pa_kernel(tc, h1, W2, b2, W3, b3, out_0, out_1):
                 op1=ALU.add,
             )
             nc.vector.tensor_scalar(out=v, in0=v, scalar1=0.0, scalar2=EPS, op0=ALU.max, op1=ALU.add)
-            for c in range(c0, c1):
-                nc.sync.dma_start(
-                    out=out_1[c * CH : (c + 1) * CH, :].rearrange("(p r) o -> p (r o)", r=R), in_=var[:, c, :]
-                )
 
         load_w(0)
         load_x(0)
@@ -399,24 +400,22 @@ def tile_gaussianmixturemlp_pa_kernel(tc, h1, W2, b2, W3, b3, out_0, out_1):
         for i in range(-2, NU):
             if i >= -1:
                 load_x(i + 5)
-            if i == 0:
-                load_bias3()
             jobs = W_JOBS.get(i, [])
             done = (i - 2) // M if (valid(i - 2) and (i - 2) % M == M - 1) else -1
-            add_bias3(i - 2)
             x_exit(i + 1, 0)
             x_exit(i + 1, 1)
             if i == -2:
                 w_prepare(jobs[0])
             x_transposes(i + 2, 0)
             x_transposes(i + 2, 1)
+            if i == 0:
+                bias3_transpose()
             if i < 1:
                 idle_plain(1)
-            hold_clock(i - 1, 2)
+            if done < 0:
+                hold_clock(i - 1, 2)
             regroup(i - 1)
             quantise1(i + 1)
-            if done >= 0:
-                mean_of(done)
             for m in jobs:
                 if i != -2 or m != jobs[0]:
                     w_prepare(m)
@@ -425,40 +424,41 @@ def tile_gaussianmixturemlp_pa_kernel(tc, h1, W2, b2, W3, b3, out_0, out_1):
                 w_quantise(m)
             if i == -2:
                 bias2()
-            if i == 1:
+            if i == 0:
                 bias3()
             nonlinear(i - 2)
             if done >= 0:
-                mean_square(done)
+                mean_of(done)
             layer1(i + 1, 0)
             h2_exit(i, 1)
             layer1(i + 1, 1)
             quantise2(i - 1)
-            layer2(i - 1)
             accumulate(i - 2)
+            layer2(i - 1)
             if done >= 0:
-                spread_sum(done)
                 spread_of(done)
             h2_exit(i, 2)
             layer1(i + 1, 2)
             h2_exit(i, 3)
             layer1(i + 1, 3)
+            if done >= 0:
+                write_out(nc.vector.tensor_copy, out_0, done, chunk[done]["mean"])
         last = NU - 1
         hold_clock(last, 3)
         regroup(last)
         quantise2(last)
-        add_bias3(last - 1)
-        layer2(last)
         nonlinear(last - 1)
-        add_bias3(last)
-        nonlinear(last)
         accumulate(last - 1)
+        layer2(last)
+        nonlinear(last)
         log_of(0, NCH - 1)
         accumulate(last)
         mean_of(NCH - 1)
-        spread_sum(NCH - 1)
-        mean_square(NCH - 1)
         log_of(NCH - 1, NCH)
         variance_of(0, NCH - 1)
+        for c in range(NCH - 1):
+            write_out(nc.scalar.copy, out_1, c, var[:, c, :])
         spread_of(NCH - 1)
         variance_of(NCH - 1, NCH)
+        write_out(nc.vector.tensor_copy, out_0, NCH - 1, chunk[NCH - 1]["mean"])
+        write_out(nc.vector.tensor_copy, out_1, NCH - 1, var[:, NCH - 1, :])

@@ -6,7 +6,6 @@ from concourse.masks import make_identity
 
 F32 = mybir.dt.float32
 BF16 = mybir.dt.bfloat16
-I32 = mybir.dt.int32
 U32 = mybir.dt.uint32
 U8 = mybir.dt.uint8
 FP8X4 = mybir.dt.float8_e4m3fn_x4
@@ -20,7 +19,6 @@ H = 512
 O = 64
 O2 = 128
 CH = 512
-HALF = CH // 2
 NCH = B // CH
 R = CH // P
 NU = NCH * M
@@ -28,12 +26,8 @@ EPS = 1e-6
 CLAMP = 14.0
 DELTA = 1.0 / (1.0 + math.exp(CLAMP))
 LN_SCALE = 2.0 ** 40
-W3W = 5 * O
 
 FLOPS = 2 * M * B * H * H + 2 * M * B * H * O2
-
-W_JOBS = {-2: [0, 1], -1: [2, 3], 0: [4]}
-VECTOR_EXITS = 3
 
 
 def tile_gaussianmixturemlp_pa_kernel(tc, h1, W2, b2, W3, b3, out_0, out_1):
@@ -41,7 +35,7 @@ def tile_gaussianmixturemlp_pa_kernel(tc, h1, W2, b2, W3, b3, out_0, out_1):
     with ExitStack() as ctx:
         const = ctx.enter_context(tc.tile_pool(name="const", bufs=1))
         keep = ctx.enter_context(tc.tile_pool(name="keep", bufs=1))
-        wraw = ctx.enter_context(tc.tile_pool(name="wraw", bufs=M))
+        wraw = ctx.enter_context(tc.tile_pool(name="wraw", bufs=2))
         xin = ctx.enter_context(tc.tile_pool(name="xin", bufs=5))
         work = ctx.enter_context(tc.tile_pool(name="work", bufs=3))
         codes = ctx.enter_context(tc.tile_pool(name="codes", bufs=3))
@@ -50,28 +44,25 @@ def tile_gaussianmixturemlp_pa_kernel(tc, h1, W2, b2, W3, b3, out_0, out_1):
         ctx.enter_context(tc.manual_schedule())
 
         ident = const.tile([P, P], F32)
-        identb = const.tile([P, P], BF16)
+        neg_clamp = const.tile([P, 1], F32)
         ones = const.tile([P, 1], F32)
         ln_shift = const.tile([P, 1], F32)
-        zeros = const.tile([P, CH], BF16)
+        acc_init = const.tile([P, 1], F32)
         b2raw = const.tile([P, M, 4], BF16)
         b2f = const.tile([P, M, 4], F32)
-        b3rows = const.tile([P, P], BF16)
-        b3col = const.tile([P, M, 2], F32)
-        neg_bv = const.tile([P, M], F32)
-        floor_x = const.tile([P, M], F32)
-        floor_sum = const.tile([P, 1], F32)
-        acc_init = const.tile([P, 1], F32)
-        b_mean = const.tile([P, 1], F32)
+        b3raw = const.tile([P, M, O2], BF16)
+        b3f = const.tile([P, M, O2], F32)
+        b3m = const.tile([P, O], F32)
+        zeros = const.tile([P, CH], BF16)
 
         w2c = keep.tile([P, M, H], U32, align_bytes=64)
         w2s = keep.tile([P, M, H], U8, align_bytes=64)
-        w3c = keep.tile([P, M, W3W], U32, align_bytes=64)
-        w3s = keep.tile([P, M, W3W], U8, align_bytes=64)
-        q_all = keep.tile([P, NCH, HALF], F32)
-        a2_all = keep.tile([P, NCH, HALF], F32)
-        lnq = keep.tile([P, NCH, HALF], F32)
-        var = keep.tile([P, NCH, HALF], F32)
+        w3c = keep.tile([P, M, O2], U32, align_bytes=64)
+        w3s = keep.tile([P, M, O2], U8, align_bytes=64)
+        q_all = keep.tile([P, NCH, R * O], F32)
+        a2_all = keep.tile([P, NCH, R * O], F32)
+        lnq = keep.tile([P, NCH, R * O], F32)
+        var = keep.tile([P, NCH, R * O], F32)
 
         unit = {}
         wt = {}
@@ -85,40 +76,37 @@ def tile_gaussianmixturemlp_pa_kernel(tc, h1, W2, b2, W3, b3, out_0, out_1):
             for k in range(n):
                 nc.tensor.matmul(out=scratch[:], lhsT=zeros[:, 0:P], rhs=zeros[:], start=True, stop=True)
 
+        def load_bias3():
+            nc.sync.dma_start(
+                out=b3raw[:].rearrange("p m o -> p (m o)"),
+                in_=b3.rearrange("m o -> (m o)").partition_broadcast(P),
+            )
+
         def setup():
             nc.vector.memset(zeros[:], 0.0)
             idle_plain(4)
             make_identity(nc, ident[:])
-            make_identity(nc, identb[:])
+            nc.vector.memset(neg_clamp[:], -CLAMP)
             nc.vector.memset(ones[:], 1.0)
-            nc.vector.memset(b3rows[:], 0.0)
-            nc.vector.memset(w3c[:].bitcast(I32), 0)
-            nc.vector.memset(w3s[:].bitcast(I32), 0)
             nc.scalar.dma_start(out=b2raw[:], in_=b2.rearrange("m (p t) -> p m t", t=4))
-            b3_rows = b3.rearrange("m (k o) -> (m k) o", k=2)
-            nc.scalar.dma_start(out=b3rows[0 : 2 * M, 0:O], in_=b3_rows)
-            nc.scalar.dma_start(out=b3rows[0 : 2 * M, O:O2], in_=b3_rows)
             nc.scalar.activation(out=ln_shift[:], in_=ones[:], func=ACT.Ln, scale=LN_SCALE)
+            nc.vector.tensor_scalar(
+                out=acc_init[:], in0=ln_shift[:], scalar1=0.5, scalar2=0.5 * M * EPS, op0=ALU.mult, op1=ALU.add
+            )
 
         def bias2():
             nc.vector.tensor_copy(out=b2f[:], in_=b2raw[:])
 
-        def bias3_transpose():
-            bank = psum.tile([P, P], BF16, tag="bank")
-            nc.tensor.transpose(bank[:], b3rows[:], identb[:])
-            nc.vector.tensor_copy(out=b3col[:].rearrange("p m k -> p (m k)"), in_=bank[:, 0 : 2 * M])
-
         def bias3():
-            nc.vector.tensor_scalar_mul(out=neg_bv[:], in0=b3col[:, :, 1], scalar1=-1.0)
-            nc.vector.tensor_scalar(
-                out=floor_x[:], in0=b3col[:, :, 1], scalar1=-1.0, scalar2=CLAMP, op0=ALU.mult, op1=ALU.add
+            nc.vector.tensor_copy(out=b3f[:, :, 0:O], in_=b3raw[:, :, 0:O])
+            nc.vector.tensor_scalar_add(out=b3f[:, :, O:O2], in0=b3raw[:, :, O:O2], scalar1=-CLAMP)
+            nc.vector.tensor_reduce(
+                out=b3m[:],
+                in_=b3f[:, :, 0:O].rearrange("p m o -> p o m"),
+                axis=mybir.AxisListType.X,
+                op=ALU.add,
             )
-            nc.vector.tensor_reduce(out=floor_sum[:], in_=floor_x[:], axis=mybir.AxisListType.X, op=ALU.add)
-            nc.vector.scalar_tensor_tensor(
-                out=acc_init[:], in0=ln_shift[:], scalar=M * EPS, in1=floor_sum[:], op0=ALU.add, op1=ALU.subtract
-            )
-            nc.vector.tensor_reduce(out=b_mean[:], in_=b3col[:, :, 0], axis=mybir.AxisListType.X, op=ALU.add)
-            nc.vector.tensor_scalar_mul(out=b_mean[:], in0=b_mean[:], scalar1=1.0 / M)
+            nc.vector.tensor_scalar_mul(out=b3m[:], in0=b3m[:], scalar1=1.0 / M)
 
         def load_w(m):
             w2raw = wraw.tile([P, 4 * H], BF16, tag="w2raw")
@@ -130,7 +118,7 @@ def tile_gaussianmixturemlp_pa_kernel(tc, h1, W2, b2, W3, b3, out_0, out_1):
         def load_x(u):
             if not valid(u):
                 return
-            c, m = divmod(u, M)
+            m, c = divmod(u, NCH)
             x = xin.tile([P, R * H], BF16, tag="x")
             nc.sync.dma_start(
                 out=x[:], in_=h1[m, c * CH : (c + 1) * CH, :].rearrange("(p r) k -> p (r k)", r=R)
@@ -149,35 +137,35 @@ def tile_gaussianmixturemlp_pa_kernel(tc, h1, W2, b2, W3, b3, out_0, out_1):
             dst = grouped[:].bitcast(F32).rearrange("q (r c w) -> q r c w", c=P, w=2)
             copy(out=dst[:, 2 * j : 2 * j + 2], in_=bank[:].rearrange("q a w c -> q a c w"))
 
-        def w_prepare(m):
+        def w_transposes(m, j):
             d = wt[m]
-            gw2 = work.tile([P, 4 * H], BF16, align_bytes=64, tag="gw2", bufs=2)
-            gw3 = work.tile([P, 4 * O2], BF16, align_bytes=64, tag="gw3", bufs=2)
-            for j in range(2):
-                bank = transpose_pair(d["w2raw"][:].bitcast(F32), j)
-                words_out(nc.scalar.copy, gw2, j, bank)
-            idle_plain(1)
-            w3w = d["w3raw"][:].bitcast(F32).rearrange("o (p w) -> o p w", w=2)
-            bank3 = psum.tile([P, 2, 2, P], F32, tag="bank")
-            for w in range(2):
-                nc.tensor.transpose(bank3[:, 0, w, :], w3w[:, :, w], ident[:])
-            nc.vector.tensor_copy(
-                out=gw3[:].bitcast(F32).rearrange("p (o w) -> p o w", w=2),
-                in_=bank3[:, 0].rearrange("p w o -> p o w"),
-            )
-            d["gw2"] = gw2
-            d["gw3"] = gw3
+            if j < 2:
+                d["tp%d" % j] = transpose_pair(d["w2raw"][:].bitcast(F32), j)
+            else:
+                w3w = d["w3raw"][:].bitcast(F32).rearrange("o (p w) -> o p w", w=2)
+                bank3 = psum.tile([P, 2, 2, P], F32, tag="bank")
+                for w in range(2):
+                    nc.tensor.transpose(bank3[:, 0, w, :], w3w[:, :, w], ident[:])
+                d["tp2"] = bank3
+
+        def w_exit(m, j):
+            d = wt[m]
+            if j == 0:
+                d["gw2"] = work.tile([P, 4 * H], BF16, align_bytes=64, tag="gw2", bufs=2, name="gw2")
+            if j < 2:
+                words_out(nc.scalar.copy if j == 1 else nc.vector.tensor_copy, d["gw2"], j, d["tp%d" % j])
+            else:
+                gw3 = work.tile([P, 4 * O2], BF16, align_bytes=64, tag="gw3", bufs=2)
+                nc.vector.tensor_copy(
+                    out=gw3[:].bitcast(F32).rearrange("p (o w) -> p o w", w=2),
+                    in_=d["tp2"][:, 0].rearrange("p w o -> p o w"),
+                )
+                d["gw3"] = gw3
 
         def w_quantise(m):
             d = wt[m]
             nc.vector.quantize_mx(out=w2c[:, m, :].bitcast(FP8X4), scales=w2s[:, m, :], in_=d["gw2"][:])
-            for k in range(2):
-                lo = (2 * k + 1) * O
-                nc.vector.quantize_mx(
-                    out=w3c[:, m, lo : lo + O].bitcast(FP8X4),
-                    scales=w3s[:, m, lo : lo + O],
-                    in_=d["gw3"][:, 4 * O * k : 4 * O * (k + 1)],
-                )
+            nc.vector.quantize_mx(out=w3c[:, m, :].bitcast(FP8X4), scales=w3s[:, m, :], in_=d["gw3"][:])
 
         def x_transposes(u, j):
             if valid(u):
@@ -205,7 +193,7 @@ def tile_gaussianmixturemlp_pa_kernel(tc, h1, W2, b2, W3, b3, out_0, out_1):
             if not valid(u):
                 return
             d = unit[u]
-            m = u % M
+            m = u // NCH
             acc1 = psum.tile([P, CH], F32, tag="bank")
             nc.tensor.matmul_mx(
                 out=acc1[:],
@@ -222,26 +210,16 @@ def tile_gaussianmixturemlp_pa_kernel(tc, h1, W2, b2, W3, b3, out_0, out_1):
             if not valid(u):
                 return
             d = unit[u]
-            m = u % M
+            m = u // NCH
             if t == 0:
                 d["planes"] = work.tile([P, 4, CH], BF16, tag="planes", name="planes")
-            if t == 3 and m < VECTOR_EXITS:
-                nc.vector.tensor_scalar(
-                    out=d["planes"][:, t, :],
-                    in0=d["l1_%d" % t][:],
-                    scalar1=b2f[:, m, t : t + 1],
-                    scalar2=0.0,
-                    op0=ALU.add,
-                    op1=ALU.max,
-                )
-            else:
-                nc.scalar.activation(
-                    out=d["planes"][:, t, :],
-                    in_=d["l1_%d" % t][:],
-                    func=ACT.Relu,
-                    bias=b2f[:, m, t : t + 1],
-                    scale=1.0,
-                )
+            nc.scalar.activation(
+                out=d["planes"][:, t, :],
+                in_=d["l1_%d" % t][:],
+                func=ACT.Relu,
+                bias=b2f[:, m, t : t + 1],
+                scale=1.0,
+            )
 
         def regroup(u):
             if not valid(u):
@@ -258,34 +236,32 @@ def tile_gaussianmixturemlp_pa_kernel(tc, h1, W2, b2, W3, b3, out_0, out_1):
             if not valid(u):
                 return
             d = unit[u]
-            c2 = codes.tile([P, CH], U32, align_bytes=64, tag="c2", bufs=8)
-            s2 = codes.tile([P, CH], U8, align_bytes=64, tag="s2", bufs=8)
+            c2 = codes.tile([P, CH], U32, align_bytes=64, tag="c2", bufs=NU)
+            s2 = codes.tile([P, CH], U8, align_bytes=64, tag="s2", bufs=NU)
             nc.vector.quantize_mx(out=c2[:].bitcast(FP8X4), scales=s2[:], in_=d["g2"][:])
             d["c2"] = c2
             d["s2"] = s2
 
-        def layer2_pair(out, u, k, start, stop):
+        def layer2_pass(out, u, r, start, stop):
             d = unit[u]
-            m = u % M
-            for h in range(2):
-                lo = 2 * O * k + O * (1 - h)
-                nc.tensor.matmul_mx(
-                    out=out,
-                    lhsT=w3c[:, m, lo : lo + P].bitcast(FP8X4),
-                    lhsT_scale=w3s[:, m, lo : lo + P],
-                    rhs=d["c2"][:, h * HALF : (h + 1) * HALF].bitcast(FP8X4),
-                    rhs_scale=d["s2"][:, h * HALF : (h + 1) * HALF],
-                    start=(start and h == 0),
-                    stop=(stop and h == 1),
-                )
+            m = u // NCH
+            nc.tensor.matmul_mx(
+                out=out,
+                lhsT=d["c2"][:, r * P : (r + 1) * P].bitcast(FP8X4),
+                lhsT_scale=d["s2"][:, r * P : (r + 1) * P],
+                rhs=w3c[:, m, :].bitcast(FP8X4),
+                rhs_scale=w3s[:, m, :],
+                start=start,
+                stop=stop,
+            )
 
         def hold_clock(u, n):
             if not valid(u):
                 return
-            pb = psum.tile([P, 2, HALF], F32, tag="bank")
+            yb = psum.tile([P, R, O2], F32, tag="bank")
             for k in range(n):
                 nc.tensor.matmul_mx(
-                    out=pb[:].rearrange("p k f -> p (k f)"),
+                    out=yb[:].rearrange("p r o -> p (r o)"),
                     lhsT=w2c[:, 0, 0:P].bitcast(FP8X4),
                     lhsT_scale=w2s[:, 0, 0:P],
                     rhs=w2c[:, 0, :].bitcast(FP8X4),
@@ -293,83 +269,106 @@ def tile_gaussianmixturemlp_pa_kernel(tc, h1, W2, b2, W3, b3, out_0, out_1):
                     start=True,
                     stop=True,
                 )
-            unit[u]["pb"] = pb
+            unit[u]["yb"] = yb
 
         def layer2(u):
             if not valid(u):
                 return
-            d = unit[u]
-            if "pb" not in d:
-                d["pb"] = psum.tile([P, 2, HALF], F32, tag="bank", name="pb")
-            for k in range(2):
-                layer2_pair(d["pb"][:, k, :], u, k, True, True)
-            if u % M == M - 1:
-                c = u // M
-                tb = psum.tile([P, 2, HALF], F32, tag="bank")
-                for m in range(M):
-                    layer2_pair(tb[:, 0, :], c * M + m, 0, m == 0, m == M - 1)
+            yb = unit[u]["yb"]
+            for r in range(R):
+                layer2_pass(yb[:, r, :], u, r, True, True)
+            if u // NCH == M - 1:
+                c = u % NCH
+                tb = psum.tile([P, R, O2], F32, tag="bank")
+                for r in range(R):
+                    for m in range(M):
+                        layer2_pass(tb[:, r, :], m * NCH + c, r, m == 0, m == M - 1)
                 chunk[c]["tb"] = tb
+
+        def add_bias3(u):
+            if not valid(u):
+                return
+            d = unit[u]
+            m = u // NCH
+            y = epi.tile([P, R, O2], F32, tag="y")
+            nc.vector.tensor_tensor(
+                out=y[:],
+                in0=d["yb"][:],
+                in1=b3f[:, m, :].unsqueeze(1).to_broadcast([P, R, O2]),
+                op=ALU.add,
+            )
+            d["y"] = y
 
         def nonlinear(u):
             if not valid(u):
                 return
             d = unit[u]
-            m = u % M
-            sq = epi.tile([P, HALF], F32, tag="sq")
-            sg = epi.tile([P, HALF], F32, tag="sg")
-            nc.scalar.activation(out=sq[:], in_=d["pb"][:, 0, :], func=ACT.Square, bias=b3col[:, m, 0:1], scale=1.0)
+            y = d["y"]
+            sg = epi.tile([P, R, O], F32, tag="sg")
             nc.scalar.activation(
-                out=sg[:], in_=d["pb"][:, 1, :], func=ACT.Sigmoid, bias=neg_bv[:, m : m + 1], scale=-1.0
+                out=sg[:], in_=y[:, :, O:O2], func=ACT.Sigmoid, bias=neg_clamp[:], scale=-1.0
             )
-            d["sq"] = sq
+            nc.scalar.activation(out=y[:, :, 0:O], in_=y[:, :, 0:O], func=ACT.Square)
             d["sg"] = sg
 
         def accumulate(u):
             if not valid(u):
                 return
             d = unit[u]
-            c, m = divmod(u, M)
+            m, c = divmod(u, NCH)
             if m == 0:
-                chunk[c] = {"acc": epi.tile([P, HALF], F32, tag="acc", bufs=2, name="acc")}
+                chunk[c] = {"acc": epi.tile([P, R, O2], F32, tag="acc", bufs=NCH, name="acc")}
             q = q_all[:, c, :]
-            acc = chunk[c]["acc"]
-            raw = d["pb"][:, 1, :]
+            sgf = d["sg"][:].rearrange("p r o -> p (r o)")
+            yf = d["y"][:].rearrange("p r o -> p (r o)")
+            accf = chunk[c]["acc"][:].rearrange("p r o -> p (r o)")
             if m == 0:
-                nc.vector.tensor_scalar_max(out=q, in0=d["sg"][:], scalar1=DELTA)
+                nc.vector.tensor_scalar_max(out=q, in0=sgf, scalar1=DELTA)
                 nc.vector.tensor_scalar(
-                    out=acc[:], in0=raw, scalar1=floor_x[:, 0:1], scalar2=acc_init[:, 0:1], op0=ALU.max, op1=ALU.add
+                    out=accf, in0=yf, scalar1=0.0, scalar2=acc_init[:, 0:1], op0=ALU.max, op1=ALU.add
                 )
             else:
-                nc.vector.scalar_tensor_tensor(out=q, in0=d["sg"][:], scalar=DELTA, in1=q, op0=ALU.max, op1=ALU.mult)
-                nc.vector.scalar_tensor_tensor(
-                    out=acc[:], in0=raw, scalar=floor_x[:, m : m + 1], in1=acc[:], op0=ALU.max, op1=ALU.add
-                )
-            nc.vector.tensor_tensor(out=acc[:], in0=acc[:], in1=d["sq"][:], op=ALU.add)
+                nc.vector.scalar_tensor_tensor(out=q, in0=sgf, scalar=DELTA, in1=q, op0=ALU.max, op1=ALU.mult)
+                nc.vector.scalar_tensor_tensor(out=accf, in0=yf, scalar=0.0, in1=accf, op0=ALU.max, op1=ALU.add)
 
         def mean_of(c):
             d = chunk[c]
-            mean = epi.tile([P, HALF], F32, tag="mean", bufs=2)
-            msq = epi.tile([P, HALF], F32, tag="msq", bufs=2)
-            nc.scalar.activation(out=mean[:], in_=d["tb"][:, 0, :], func=ACT.Identity, bias=b_mean[:], scale=1.0 / M)
-            nc.scalar.activation(out=msq[:], in_=d["tb"][:, 0, :], func=ACT.Square, bias=b_mean[:], scale=1.0 / M)
+            mean = epi.tile([P, R, O], F32, tag="mean", bufs=2)
+            nc.vector.scalar_tensor_tensor(
+                out=mean[:],
+                in0=d["tb"][:, :, 0:O],
+                scalar=1.0 / M,
+                in1=b3m[:].unsqueeze(1).to_broadcast([P, R, O]),
+                op0=ALU.mult,
+                op1=ALU.add,
+            )
+            nc.sync.dma_start(
+                out=out_0[c * CH : (c + 1) * CH, :].rearrange("(p r) o -> p (r o)", r=R),
+                in_=mean[:].rearrange("p r o -> p (r o)"),
+            )
             d["mean"] = mean
+
+        def mean_square(c):
+            d = chunk[c]
+            msq = epi.tile([P, R, O], F32, tag="msq", bufs=2)
+            nc.scalar.activation(out=msq[:], in_=d["mean"][:], func=ACT.Square)
             d["msq"] = msq
+
+        def spread_sum(c):
+            d = chunk[c]
+            a1 = epi.tile([P, R, O], F32, tag="a1", bufs=2)
+            nc.vector.tensor_tensor(out=a1[:], in0=d["acc"][:, :, 0:O], in1=d["acc"][:, :, O:O2], op=ALU.add)
+            d["a1"] = a1
 
         def spread_of(c):
             d = chunk[c]
             nc.vector.scalar_tensor_tensor(
-                out=a2_all[:, c, :], in0=d["acc"][:], scalar=1.0 / M, in1=d["msq"][:], op0=ALU.mult, op1=ALU.subtract
-            )
-
-        def write_out(copy, dram, c, src):
-            bank = psum.tile([P, 2, P], F32, tag="bank")
-            for k in range(2):
-                nc.tensor.transpose(bank[:, k, :], src[:, k * P : (k + 1) * P], ident[:])
-            res = epi.tile([P, 2, 2, O], F32, tag="res", bufs=3)
-            copy(out=res[:], in_=bank[:].rearrange("p k (h o) -> p h k o", h=2))
-            nc.sync.dma_start(
-                out=dram[c * CH : (c + 1) * CH, :].rearrange("(p r) o -> p (r o)", r=R),
-                in_=res[:].rearrange("p h k o -> p (h k o)"),
+                out=a2_all[:, c, :],
+                in0=d["a1"][:].rearrange("p r o -> p (r o)"),
+                scalar=1.0 / M,
+                in1=d["msq"][:].rearrange("p r o -> p (r o)"),
+                op0=ALU.mult,
+                op1=ALU.subtract,
             )
 
         def log_of(c0, c1):
@@ -386,79 +385,91 @@ def tile_gaussianmixturemlp_pa_kernel(tc, h1, W2, b2, W3, b3, out_0, out_1):
                 op1=ALU.add,
             )
             nc.vector.tensor_scalar(out=v, in0=v, scalar1=0.0, scalar2=EPS, op0=ALU.max, op1=ALU.add)
+            for c in range(c0, c1):
+                nc.sync.dma_start(
+                    out=out_1[c * CH : (c + 1) * CH, :].rearrange("(p r) o -> p (r o)", r=R), in_=var[:, c, :]
+                )
 
         load_w(0)
         load_x(0)
         setup()
-        load_w(1)
         load_x(1)
-        load_w(2)
-        load_w(3)
         load_x(2)
-        load_w(4)
-        load_x(3)
         for i in range(-2, NU):
             if i >= -1:
-                load_x(i + 5)
-            jobs = W_JOBS.get(i, [])
-            done = (i - 2) // M if (valid(i - 2) and (i - 2) % M == M - 1) else -1
+                load_x(i + 4)
+            if i == 0:
+                load_bias3()
+            if i == -2:
+                load_w(1)
+            elif i % NCH == 1 and i // NCH + 2 < M:
+                load_w(i // NCH + 2)
+            piece = (i // NCH + 1, i % NCH) if (i >= 0 and i % NCH < 3 and i // NCH + 1 < M) else None
+            done = (i - 2) % NCH if (valid(i - 2) and (i - 2) // NCH == M - 1) else -1
+            add_bias3(i - 2)
             x_exit(i + 1, 0)
             x_exit(i + 1, 1)
             if i == -2:
-                w_prepare(jobs[0])
+                for j in range(3):
+                    w_transposes(0, j)
+                    w_exit(0, j)
             x_transposes(i + 2, 0)
             x_transposes(i + 2, 1)
-            if i == 0:
-                bias3_transpose()
+            if piece:
+                w_transposes(piece[0], piece[1])
             if i < 1:
                 idle_plain(1)
-            if done < 0:
-                hold_clock(i - 1, 2)
+            hold_clock(i - 1, 2)
             regroup(i - 1)
             quantise1(i + 1)
-            for m in jobs:
-                if i != -2 or m != jobs[0]:
-                    w_prepare(m)
+            if done >= 0:
+                mean_of(done)
             h2_exit(i, 0)
-            for m in jobs:
-                w_quantise(m)
+            if piece:
+                w_exit(piece[0], piece[1])
+                if piece[1] == 2:
+                    w_quantise(piece[0])
             if i == -2:
+                w_quantise(0)
                 bias2()
-            if i == 0:
+            if i == 1:
                 bias3()
             nonlinear(i - 2)
             if done >= 0:
-                mean_of(done)
+                mean_square(done)
             layer1(i + 1, 0)
             h2_exit(i, 1)
             layer1(i + 1, 1)
             quantise2(i - 1)
-            accumulate(i - 2)
             layer2(i - 1)
+            accumulate(i - 2)
             if done >= 0:
+                spread_sum(done)
                 spread_of(done)
             h2_exit(i, 2)
             layer1(i + 1, 2)
             h2_exit(i, 3)
             layer1(i + 1, 3)
-            if done >= 0:
-                write_out(nc.vector.tensor_copy, out_0, done, chunk[done]["mean"])
         last = NU - 1
         hold_clock(last, 3)
         regroup(last)
         quantise2(last)
-        nonlinear(last - 1)
-        accumulate(last - 1)
+        add_bias3(last - 1)
+        mean_of(NCH - 2)
         layer2(last)
+        nonlinear(last - 1)
+        mean_square(NCH - 2)
+        add_bias3(last)
         nonlinear(last)
-        log_of(0, NCH - 1)
+        accumulate(last - 1)
+        log_of(0, NCH - 2)
+        spread_sum(NCH - 2)
+        spread_of(NCH - 2)
         accumulate(last)
         mean_of(NCH - 1)
-        log_of(NCH - 1, NCH)
-        variance_of(0, NCH - 1)
-        for c in range(NCH - 1):
-            write_out(nc.scalar.copy, out_1, c, var[:, c, :])
+        spread_sum(NCH - 1)
+        mean_square(NCH - 1)
+        log_of(NCH - 2, NCH)
+        variance_of(0, NCH - 2)
         spread_of(NCH - 1)
-        variance_of(NCH - 1, NCH)
-        write_out(nc.vector.tensor_copy, out_0, NCH - 1, chunk[NCH - 1]["mean"])
-        write_out(nc.vector.tensor_copy, out_1, NCH - 1, var[:, NCH - 1, :])
+        variance_of(NCH - 2, NCH)

@@ -47,6 +47,7 @@ def tile_gaussianmixturemlp_pa_kernel(tc, h1, W2, b2, W3, b3, out_0, out_1):
         neg_clamp = const.tile([P, 1], F32)
         ones = const.tile([P, 1], F32)
         ln_shift = const.tile([P, 1], F32)
+        table_warm = const.tile([P, 1], F32)
         acc_init = const.tile([P, 1], F32)
         b2raw = const.tile([P, M, 4], BF16)
         b2f = const.tile([P, M, 4], F32)
@@ -90,6 +91,7 @@ def tile_gaussianmixturemlp_pa_kernel(tc, h1, W2, b2, W3, b3, out_0, out_1):
             nc.vector.memset(ones[:], 1.0)
             nc.scalar.dma_start(out=b2raw[:], in_=b2.rearrange("m (p t) -> p m t", t=4))
             nc.scalar.activation(out=ln_shift[:], in_=ones[:], func=ACT.Ln, scale=LN_SCALE)
+            nc.scalar.activation(out=table_warm[:], in_=ones[:], func=ACT.Sigmoid)
             nc.vector.tensor_scalar(
                 out=acc_init[:], in0=ln_shift[:], scalar1=0.5, scalar2=0.5 * M * EPS, op0=ALU.mult, op1=ALU.add
             )

import math
from contextlib import ExitStack

import concourse.mybir as mybir
from concourse.masks import make_identity

F32 = mybir.dt.float32
BF16 = mybir.dt.bfloat16
U32 = mybir.dt.uint32
U8 = mybir.dt.uint8
FP8X4 = mybir.dt.float8_e4m3fn_x4
ALU = mybir.AluOpType
ACT = mybir.ActivationFunctionType

P = 128
M = 5
B = 2048
H = 512
O = 64
O2 = 128
CH = 512
NCH = B // CH
R = CH // P
NU = NCH * M
EPS = 1e-6
CLAMP = 14.0
DELTA = 1.0 / (1.0 + math.exp(CLAMP))
LN_SCALE = 2.0 ** 40

FLOPS = 2 * M * B * H * H + 2 * M * B * H * O2


def tile_gaussianmixturemlp_pa_kernel(tc, h1, W2, b2, W3, b3, out_0, out_1):
    nc = tc.nc
    with ExitStack() as ctx:
        const = ctx.enter_context(tc.tile_pool(name="const", bufs=1))
        keep = ctx.enter_context(tc.tile_pool(name="keep", bufs=1))
        wraw = ctx.enter_context(tc.tile_pool(name="wraw", bufs=2))
        xin = ctx.enter_context(tc.tile_pool(name="xin", bufs=5))
        work = ctx.enter_context(tc.tile_pool(name="work", bufs=3))
        codes = ctx.enter_context(tc.tile_pool(name="codes", bufs=3))
        epi = ctx.enter_context(tc.tile_pool(name="epi", bufs=3))
        psum = ctx.enter_context(tc.psum_pool(name="psum", bufs=8))
        ctx.enter_context(tc.manual_schedule())

        ident = const.tile([P, P], F32)
        neg_clamp = const.tile([P, 1], F32)
        ones = const.tile([P, 1], F32)
        ln_shift = const.tile([P, 1], F32)
        table_warm = const.tile([P, 1], F32)
        acc_init = const.tile([P, 1], F32)
        b2raw = const.tile([P, M, 4], BF16)
        b2f = const.tile([P, M, 4], F32)
        b3raw = const.tile([P, M, O2], BF16)
        b3f = const.tile([P, M, O2], F32)
        b3m = const.tile([P, O], F32)
        zeros = const.tile([P, CH], BF16)

        w2c = keep.tile([P, M, H], U32, align_bytes=64)
        w2s = keep.tile([P, M, H], U8, align_bytes=64)
        w3c = keep.tile([P, M, O2], U32, align_bytes=64)
        w3s = keep.tile([P, M, O2], U8, align_bytes=64)
        q_all = keep.tile([P, NCH, R * O], F32)
        a2_all = keep.tile([P, NCH, R * O], F32)
        lnq = keep.tile([P, NCH, R * O], F32)
        var = keep.tile([P, NCH, R * O], F32)

        unit = {}
        wt = {}
        chunk = {}

        def valid(u):
            return 0 <= u < NU

        def idle_plain(n):
            scratch = psum.tile([P, CH], F32, tag="bank")
            for k in range(n):
                nc.tensor.matmul(out=scratch[:], lhsT=zeros[:, 0:P], rhs=zeros[:], start=True, stop=True)

        def load_bias3():
            nc.sync.dma_start(
                out=b3raw[:].rearrange("p m o -> p (m o)"),
                in_=b3.rearrange("m o -> (m o)").partition_broadcast(P),
            )

        def setup():
            nc.vector.memset(zeros[:], 0.0)
            idle_plain(4)
            make_identity(nc, ident[:])
            nc.vector.memset(neg_clamp[:], -CLAMP)
            nc.vector.memset(ones[:], 1.0)
            nc.scalar.dma_start(out=b2raw[:], in_=b2.rearrange("m (p t) -> p m t", t=4))
            nc.scalar.activation(out=ln_shift[:], in_=ones[:], func=ACT.Ln, scale=LN_SCALE)
            nc.scalar.activation(out=table_warm[:], in_=ones[:], func=ACT.Sigmoid)
            nc.vector.tensor_scalar(
                out=acc_init[:], in0=ln_shift[:], scalar1=0.5, scalar2=0.5 * M * EPS, op0=ALU.mult, op1=ALU.add
            )

        def bias2():
            nc.vector.tensor_copy(out=b2f[:], in_=b2raw[:])

        def bias3():
            nc.vector.tensor_copy(out=b3f[:, :, 0:O], in_=b3raw[:, :, 0:O])
            nc.vector.tensor_scalar_add(out=b3f[:, :, O:O2], in0=b3raw[:, :, O:O2], scalar1=-CLAMP)
            nc.vector.tensor_reduce(
                out=b3m[:],
                in_=b3f[:, :, 0:O].rearrange("p m o -> p o m"),
                axis=mybir.AxisListType.X,
                op=ALU.add,
            )
            nc.vector.tensor_scalar_mul(out=b3m[:], in0=b3m[:], scalar1=1.0 / M)

        def load_w(m):
            w2raw = wraw.tile([P, 4 * H], BF16, tag="w2raw")
            nc.sync.dma_start(out=w2raw[:], in_=W2[m].rearrange("(p t) k -> p (t k)", t=4))
            w3raw = wraw.tile([P, H], BF16, tag="w3raw")
            nc.sync.dma_start(out=w3raw[:], in_=W3[m])
            wt[m] = {"w2raw": w2raw, "w3raw": w3raw}

        def load_x(u):
            if not valid(u):
                return
            m, c = divmod(u, NCH)
            x = xin.tile([P, R * H], BF16, tag="x")
            nc.sync.dma_start(
                out=x[:], in_=h1[m, c * CH : (c + 1) * CH, :].rearrange("(p r) k -> p (r k)", r=R)
            )
            unit[u] = {"x": x}

        def transpose_pair(src_words, j):
            bank = psum.tile([P, 2, 2, P], F32, tag="bank")
            for a in range(2):
                for w in range(2):
                    off = (2 * j + a) * 256 + w * P
                    nc.tensor.transpose(bank[:, a, w, :], src_words[:, off : off + P], ident[:])
            return bank

        def words_out(copy, grouped, j, bank):
            dst = grouped[:].bitcast(F32).rearrange("q (r c w) -> q r c w", c=P, w=2)
            copy(out=dst[:, 2 * j : 2 * j + 2], in_=bank[:].rearrange("q a w c -> q a c w"))

        def w_transposes(m, j):
            d = wt[m]
            if j < 2:
                d["tp%d" % j] = transpose_pair(d["w2raw"][:].bitcast(F32), j)
            else:
                w3w = d["w3raw"][:].bitcast(F32).rearrange("o (p w) -> o p w", w=2)
                bank3 = psum.tile([P, 2, 2, P], F32, tag="bank")
                for w in range(2):
                    nc.tensor.transpose(bank3[:, 0, w, :], w3w[:, :, w], ident[:])
                d["tp2"] = bank3

        def w_exit(m, j):
            d = wt[m]
            if j == 0:
                d["gw2"] = work.tile([P, 4 * H], BF16, align_bytes=64, tag="gw2", bufs=2, name="gw2")
            if j < 2:
                words_out(nc.scalar.copy if j == 1 else nc.vector.tensor_copy, d["gw2"], j, d["tp%d" % j])
            else:
                gw3 = work.tile([P, 4 * O2], BF16, align_bytes=64, tag="gw3", bufs=2)
                nc.vector.tensor_copy(
                    out=gw3[:].bitcast(F32).rearrange("p (o w) -> p o w", w=2),
                    in_=d["tp2"][:, 0].rearrange("p w o -> p o w"),
                )
                d["gw3"] = gw3

        def w_quantise(m):
            d = wt[m]
            nc.vector.quantize_mx(out=w2c[:, m, :].bitcast(FP8X4), scales=w2s[:, m, :], in_=d["gw2"][:])
            nc.vector.quantize_mx(out=w3c[:, m, :].bitcast(FP8X4), scales=w3s[:, m, :], in_=d["gw3"][:])

        def x_transposes(u, j):
            if valid(u):
                unit[u]["tp%d" % j] = transpose_pair(unit[u]["x"][:].bitcast(F32), j)

        def x_exit(u, j):
            if not valid(u):
                return
            d = unit[u]
            if j == 0:
                d["g1"] = work.tile([P, 4 * CH], BF16, align_bytes=64, tag="g1", name="g1")
            words_out(nc.scalar.copy, d["g1"], j, d["tp%d" % j])

        def quantise1(u):
            if not valid(u):
                return
            d = unit[u]
            c1 = codes.tile([P, CH], U32, align_bytes=64, tag="c1")
            s1 = codes.tile([P, CH], U8, align_bytes=64, tag="s1")
            nc.vector.quantize_mx(out=c1[:].bitcast(FP8X4), scales=s1[:], in_=d["g1"][:])
            d["c1"] = c1
            d["s1"] = s1

        def layer1(u, t):
            if not valid(u):
                return
            d = unit[u]
            m = u // NCH
            acc1 = psum.tile([P, CH], F32, tag="bank")
            nc.tensor.matmul_mx(
                out=acc1[:],
                lhsT=w2c[:, m, t * P : (t + 1) * P].bitcast(FP8X4),
                lhsT_scale=w2s[:, m, t * P : (t + 1) * P],
                rhs=d["c1"][:].bitcast(FP8X4),
                rhs_scale=d["s1"][:],
                start=True,
                stop=True,
            )
            d["l1_%d" % t] = acc1

        def h2_exit(u, t):
            if not valid(u):
                return
            d = unit[u]
            m = u // NCH
            if t == 0:
                d["planes"] = work.tile([P, 4, CH], BF16, tag="planes", name="planes")
            nc.scalar.activation(
                out=d["planes"][:, t, :],
                in_=d["l1_%d" % t][:],
                func=ACT.Relu,
                bias=b2f[:, m, t : t + 1],
                scale=1.0,
            )

        def regroup(u):
            if not valid(u):
                return
            d = unit[u]
            g2 = work.tile([P, 4 * CH], BF16, align_bytes=64, tag="g2")
            nc.vector.tensor_copy(
                out=g2[:].rearrange("p (c i t) -> p c t i", i=4, t=4),
                in_=d["planes"][:].rearrange("p t (c i) -> p c t i", i=4),
            )
            d["g2"] = g2

        def quantise2(u):
            if not valid(u):
                return
            d = unit[u]
            c2 = codes.tile([P, CH], U32, align_bytes=64, tag="c2", bufs=NU)
            s2 = codes.tile([P, CH], U8, align_bytes=64, tag="s2", bufs=NU)
            nc.vector.quantize_mx(out=c2[:].bitcast(FP8X4), scales=s2[:], in_=d["g2"][:])
            d["c2"] = c2
            d["s2"] = s2

        def layer2_pass(out, u, r, start, stop):
            d = unit[u]
            m = u // NCH
            nc.tensor.matmul_mx(
                out=out,
                lhsT=d["c2"][:, r * P : (r + 1) * P].bitcast(FP8X4),
                lhsT_scale=d["s2"][:, r * P : (r + 1) * P],
                rhs=w3c[:, m, :].bitcast(FP8X4),
                rhs_scale=w3s[:, m, :],
                start=start,
                stop=stop,
            )

        def hold_clock(u, n):
            if not valid(u):
                return
            yb = psum.tile([P, R, O2], F32, tag="bank")
            for k in range(n):
                nc.tensor.matmul_mx(
                    out=yb[:].rearrange("p r o -> p (r o)"),
                    lhsT=w2c[:, 0, 0:P].bitcast(FP8X4),
                    lhsT_scale=w2s[:, 0, 0:P],
                    rhs=w2c[:, 0, :].bitcast(FP8X4),
                    rhs_scale=w2s[:, 0, :],
                    start=True,
                    stop=True,
                )
            unit[u]["yb"] = yb

        def layer2(u):
            if not valid(u):
                return
            yb = unit[u]["yb"]
            for r in range(R):
                layer2_pass(yb[:, r, :], u, r, True, True)
            if u // NCH == M - 1:
                c = u % NCH
                tb = psum.tile([P, R, O2], F32, tag="bank")
                for r in range(R):
                    for m in range(M):
                        layer2_pass(tb[:, r, :], m * NCH + c, r, m == 0, m == M - 1)
                chunk[c]["tb"] = tb

        def add_bias3(u):
            if not valid(u):
                return
            d = unit[u]
            m = u // NCH
            y = epi.tile([P, R, O2], F32, tag="y")
            nc.vector.tensor_tensor(
                out=y[:],
                in0=d["yb"][:],
                in1=b3f[:, m, :].unsqueeze(1).to_broadcast([P, R, O2]),
                op=ALU.add,
            )
            d["y"] = y

        def nonlinear(u):
            if not valid(u):
                return
            d = unit[u]
            y = d["y"]
            sg = epi.tile([P, R, O], F32, tag="sg")
            nc.scalar.activation(
                out=sg[:], in_=y[:, :, O:O2], func=ACT.Sigmoid, bias=neg_clamp[:], scale=-1.0
            )
            nc.scalar.activation(out=y[:, :, 0:O], in_=y[:, :, 0:O], func=ACT.Square)
            d["sg"] = sg

        def accumulate(u):
            if not valid(u):
                return
            d = unit[u]
            m, c = divmod(u, NCH)
            if m == 0:
                chunk[c] = {"acc": epi.tile([P, R, O2], F32, tag="acc", bufs=NCH, name="acc")}
            q = q_all[:, c, :]
            sgf = d["sg"][:].rearrange("p r o -> p (r o)")
            yf = d["y"][:].rearrange("p r o -> p (r o)")
            accf = chunk[c]["acc"][:].rearrange("p r o -> p (r o)")
            if m == 0:
                nc.vector.tensor_scalar_max(out=q, in0=sgf, scalar1=DELTA)
                nc.vector.tensor_scalar(
                    out=accf, in0=yf, scalar1=0.0, scalar2=acc_init[:, 0:1], op0=ALU.max, op1=ALU.add
                )
            else:
                nc.vector.scalar_tensor_tensor(out=q, in0=sgf, scalar=DELTA, in1=q, op0=ALU.max, op1=ALU.mult)
                nc.vector.scalar_tensor_tensor(out=accf, in0=yf, scalar=0.0, in1=accf, op0=ALU.max, op1=ALU.add)

        def mean_of(c):
            d = chunk[c]
            mean = epi.tile([P, R, O], F32, tag="mean", bufs=2)
            nc.vector.scalar_tensor_tensor(
                out=mean[:],
                in0=d["tb"][:, :, 0:O],
                scalar=1.0 / M,
                in1=b3m[:].unsqueeze(1).to_broadcast([P, R, O]),
                op0=ALU.mult,
                op1=ALU.add,
            )
            nc.sync.dma_start(
                out=out_0[c * CH : (c + 1) * CH, :].rearrange("(p r) o -> p (r o)", r=R),
                in_=mean[:].rearrange("p r o -> p (r o)"),
            )
            d["mean"] = mean

        def mean_square(c):
            d = chunk[c]
            msq = epi.tile([P, R, O], F32, tag="msq", bufs=2)
            nc.scalar.activation(out=msq[:], in_=d["mean"][:], func=ACT.Square)
            d["msq"] = msq

        def spread_sum(c):
            d = chunk[c]
            a1 = epi.tile([P, R, O], F32, tag="a1", bufs=2)
            nc.vector.tensor_tensor(out=a1[:], in0=d["acc"][:, :, 0:O], in1=d["acc"][:, :, O:O2], op=ALU.add)
            d["a1"] = a1

        def spread_of(c):
            d = chunk[c]
            nc.vector.scalar_tensor_tensor(
                out=a2_all[:, c, :],
                in0=d["a1"][:].rearrange("p r o -> p (r o)"),
                scalar=1.0 / M,
                in1=d["msq"][:].rearrange("p r o -> p (r o)"),
                op0=ALU.mult,
                op1=ALU.subtract,
            )

        def log_of(c0, c1):
            nc.scalar.activation(out=lnq[:, c0:c1, :], in_=q_all[:, c0:c1, :], func=ACT.Ln, scale=LN_SCALE)

        def variance_of(c0, c1):
            v = var[:, c0:c1, :].rearrange("p c f -> p (c f)")
            nc.vector.scalar_tensor_tensor(
                out=v,
                in0=lnq[:, c0:c1, :].rearrange("p c f -> p (c f)"),
                scalar=-1.0 / M,
                in1=a2_all[:, c0:c1, :].rearrange("p c f -> p (c f)"),
                op0=ALU.mult,
                op1=ALU.add,
            )
            nc.vector.tensor_scalar(out=v, in0=v, scalar1=0.0, scalar2=EPS, op0=ALU.max, op1=ALU.add)
            for c in range(c0, c1):
                nc.sync.dma_start(
                    out=out_1[c * CH : (c + 1) * CH, :].rearrange("(p r) o -> p (r o)", r=R), in_=var[:, c, :]
                )

        load_w(0)
        load_x(0)
        setup()
        load_x(1)
        load_x(2)
        for i in range(-2, NU):
            if i >= -1:
                load_x(i + 4)
            if i == 0:
                load_bias3()
            if i == -2:
                load_w(1)
            elif i % NCH == 1 and i // NCH + 2 < M:
                load_w(i // NCH + 2)
            piece = (i // NCH + 1, i % NCH) if (i >= 0 and i % NCH < 3 and i // NCH + 1 < M) else None
            done = (i - 2) % NCH if (valid(i - 2) and (i - 2) // NCH == M - 1) else -1
            add_bias3(i - 2)
            x_exit(i + 1, 0)
            x_exit(i + 1, 1)
            if i == -2:
                for j in range(3):
                    w_transposes(0, j)
                    w_exit(0, j)
            x_transposes(i + 2, 0)
            x_transposes(i + 2, 1)
            if piece:
                w_transposes(piece[0], piece[1])
            if i < 1:
                idle_plain(1)
            hold_clock(i - 1, 2)
            regroup(i - 1)
            quantise1(i + 1)
            if done >= 0:
                mean_of(done)
            h2_exit(i, 0)
            if piece:
                w_exit(piece[0], piece[1])
                if piece[1] == 2:
                    w_quantise(piece[0])
            if i == -2:
                w_quantise(0)
                bias2()
            if i == 1:
                bias3()
            nonlinear(i - 2)
            if done >= 0:
                mean_square(done)
            layer1(i + 1, 0)
            h2_exit(i, 1)
            layer1(i + 1, 1)
            quantise2(i - 1)
            layer2(i - 1)
            accumulate(i - 2)
            if done >= 0:
                spread_sum(done)
                spread_of(done)
            h2_exit(i, 2)
            layer1(i + 1, 2)
            h2_exit(i, 3)
            layer1(i + 1, 3)
        last = NU - 1
        hold_clock(last, 3)
        regroup(last)
        quantise2(last)
        add_bias3(last - 1)
        mean_of(NCH - 2)
        layer2(last)
        nonlinear(last - 1)
        mean_square(NCH - 2)
        add_bias3(last)
        nonlinear(last)
        accumulate(last - 1)
        log_of(0, NCH - 2)
        spread_sum(NCH - 2)
        spread_of(NCH - 2)
        accumulate(last)
        mean_of(NCH - 1)
        spread_sum(NCH - 1)
        mean_square(NCH - 1)
        log_of(NCH - 2, NCH)
        variance_of(0, NCH - 2)
        spread_of(NCH - 1)
        variance_of(NCH - 2, NCH)
